import numpy as np
import ml_dtypes


def mxq(x, axis, fmt="e4m3"):
    dtype, down = {"e4m3": (ml_dtypes.float8_e4m3fn, 7), "e5m2": (ml_dtypes.float8_e5m2, 14)}[fmt]
    v = np.moveaxis(np.asarray(x, np.float32).astype(ml_dtypes.bfloat16).astype(np.float64), axis, -1)
    blocks = v.reshape(v.shape[:-1] + (-1, 32))
    amax = np.abs(blocks).max(-1, keepdims=True)
    byte = np.maximum(np.where(amax > 0, np.frexp(amax)[1] - 1 + 127, 0) - down, 1)
    scale = np.exp2(byte - 127.0)
    codes = (blocks / scale).astype(np.float32).astype(dtype).astype(np.float64)
    return np.moveaxis((codes * scale).reshape(v.shape), -1, axis)


WIDE = False


def mx_kscale(k):
    if not WIDE:
        return np.ones(k)
    levels = np.array([10, -10, 5, -5, 0])
    a = np.random.permutation(np.resize(levels, k // 512 * 4)).reshape(k // 512, 4)
    idx = np.arange(k)
    return np.exp2(a[idx // 512, idx % 128 // 32])


BF16 = ml_dtypes.bfloat16


def bf(x):
    return np.asarray(x, np.float32).astype(BF16)


def f64(x):
    return np.asarray(x).astype(np.float64)


T, B, E, H, K = 4096, 2, 512, 16, 16
R = E // H
PAD_L = K // 2


def softmax_last(z):
    e = np.exp(z - z.max(-1, keepdims=True))
    return e / e.sum(-1, keepdims=True)


def setup_inputs():
    a, s = mx_kscale(E), mx_kscale(E)
    return {
        "v": bf(np.random.standard_normal((T, B, E)) * s),
        "attn_out": bf(np.random.standard_normal((T, B, E)) * 0.3 * a),
        "dyn_w": bf(np.random.standard_normal((H * K, E)) / np.sqrt(E) / s),
        "dyn_b": bf(np.random.standard_normal(H * K) * 0.1),
        "out_proj_w": bf(np.random.standard_normal((E, 2 * E)) * 1.5 / np.sqrt(E) / np.concatenate([a, s])),
        "out_proj_b": bf(np.random.standard_normal(E) * 0.1),
    }


def reference(v, attn_out, dyn_w, dyn_b, out_proj_w, out_proj_b):
    v = f64(v)
    logits = (mxq(v, 2, "e4m3") @ mxq(f64(dyn_w), 1, "e4m3").T) + f64(dyn_b)
    w = softmax_last(logits.reshape(T, B, H, K))
    xh = np.pad(v, ((PAD_L, K - 1 - PAD_L), (0, 0), (0, 0))).reshape(T + K - 1, B, H, R)
    conv = np.zeros((T, B, H, R))
    for k in range(K):
        conv = conv + w[..., k:k + 1] * xh[k:k + T]
    cat = np.concatenate([f64(attn_out), conv.reshape(T, B, E)], axis=-1)
    return (mxq(cat, 2, "e4m3") @ mxq(f64(out_proj_w), 1, "e4m3").T) + f64(out_proj_b)

@@ -1,0 +1,245 @@
+from contextlib import ExitStack
+
+import concourse.mybir as mybir
+from concourse.masks import make_identity
+
+F32 = mybir.dt.float32
+BF16 = mybir.dt.bfloat16
+U32 = mybir.dt.uint32
+U8 = mybir.dt.uint8
+FP8X4 = mybir.dt.float8_e4m3fn_x4
+ALU = mybir.AluOpType
+ACT = mybir.ActivationFunctionType
+AXIS_X = mybir.AxisListType.X
+
+T, B, E, H, K = 4096, 2, 512, 16, 16
+R = E // H
+P = 128
+PACK = 4
+LC = T // P
+PAD_L = K // 2
+PAD_R = K - 1 - PAD_L
+WIN = LC + K - 1
+CHUNKS = E // P
+HEADS_PER_CHUNK = P // R
+WORDS = E // 2
+J_ATTN = 4
+J_OUT = 2
+V_ROWS = 8
+
+FLOPS = 2 * T * B * (E * H * K + 2 * E * E + E * K)
+
+
+def transpose_words(nc, bank, rows_as_words, ident_f32):
+    for u in range(2):
+        nc.tensor.transpose(bank[:, u, :], rows_as_words[:, u * P : (u + 1) * P], ident_f32[:])
+
+
+def tile_multiheadattention820_pa_t_kernel(tc, v, attn_out, dyn_w, dyn_b, out_proj_w, out_proj_b, out):
+    nc = tc.nc
+    v_rows = v.rearrange("(p l) b e -> p l b e", l=LC)
+    attn_rows = attn_out.rearrange("(p l) b e -> p l b e", l=LC)
+    out_rows = out.rearrange("(p l) b o -> p l b o", l=LC)
+
+    with ExitStack() as ctx:
+        keep = ctx.enter_context(tc.tile_pool(name="keep", bufs=1))
+
+        v_sb = keep.tile([P, WIN, B, E], BF16)
+        nc.gpsimd.memset(v_sb[0:1, 0:PAD_L, :, :], 0.0)
+        nc.gpsimd.memset(v_sb[96:P, PAD_L + LC : WIN, :, :], 0.0)
+
+        dw_raw = keep.tile([P, 2, E], BF16)
+        nc.sync.dma_start(out=dw_raw[:], in_=dyn_w.rearrange("(g p) e -> p g e", p=P))
+        nc.sync.dma_start(out=v_sb[1:113, 0:PAD_L, :, :], in_=v_rows[0:112, LC - PAD_L : LC, :, :])
+        nc.sync.dma_start(out=v_sb[113:P, 0:PAD_L, :, :], in_=v_rows[112 : P - 1, LC - PAD_L : LC, :, :])
+        nc.sync.dma_start(out=v_sb[:, PAD_L : PAD_L + V_ROWS, :, :], in_=v_rows[:, 0:V_ROWS, :, :])
+        db_raw = keep.tile([P, H * K], BF16)
+        nc.sync.dma_start(out=db_raw[:], in_=dyn_b.partition_broadcast(P))
+        ow_raw = keep.tile([P, CHUNKS, 2 * E], BF16)
+        nc.sync.dma_start(out=ow_raw[:], in_=out_proj_w.rearrange("(g p) k -> p g k", p=P))
+        ob_raw = keep.tile([P, E], BF16)
+        nc.sync.dma_start(out=ob_raw[:], in_=out_proj_b.partition_broadcast(P))
+        for l0 in range(V_ROWS, LC, V_ROWS):
+            nc.sync.dma_start(
+                out=v_sb[:, PAD_L + l0 : PAD_L + l0 + V_ROWS, :, :], in_=v_rows[:, l0 : l0 + V_ROWS, :, :]
+            )
+        nc.sync.dma_start(out=v_sb[0:112, PAD_L + LC : WIN, :, :], in_=v_rows[1:113, 0:PAD_R, :, :])
+        nc.sync.dma_start(out=v_sb[112 : P - 1, PAD_L + LC : WIN, :, :], in_=v_rows[113:P, 0:PAD_R, :, :])
+
+        ident_f32 = keep.tile([P, P], F32)
+        make_identity(nc, ident_f32[:])
+        ident_bf16 = keep.tile([P, P], BF16)
+        make_identity(nc, ident_bf16[:])
+
+        dw_codes = keep.tile([P, H * K], U32, align_bytes=64)
+        dw_scales = keep.tile([P, H * K], U8, align_bytes=64)
+        w1_codes = keep.tile([P, E], U32, align_bytes=64)
+        w1_scales = keep.tile([P, E], U8, align_bytes=64)
+        w2_codes = keep.tile([P, E], U32, align_bytes=64)
+        w2_scales = keep.tile([P, E], U8, align_bytes=64)
+        dyn_bias = keep.tile([P, H * K], F32)
+        out_bias = keep.tile([P, E], F32)
+        nc.vector.tensor_copy(out=dyn_bias[:], in_=db_raw[:])
+        nc.vector.tensor_copy(out=out_bias[:], in_=ob_raw[:])
+
+        with tc.tile_pool(name="prep", bufs=1) as prep, tc.psum_pool(name="prep_ps", bufs=2) as prep_ps:
+            dw_grp = prep.tile([P, H * K, PACK], BF16, align_bytes=64)
+            dw_words = dw_raw[:].bitcast(F32)
+            dw_bank = prep_ps.tile([P, 2, 2 * P], F32, tag="words")
+            for g in range(2):
+                transpose_words(nc, dw_bank[:, :, g * P : (g + 1) * P], dw_words[:, g, :], ident_f32)
+            nc.vector.tensor_copy(out=dw_grp[:].bitcast(F32), in_=dw_bank[:].rearrange("q u n -> q n u"))
+            nc.vector.quantize_mx(
+                out=dw_codes[:].bitcast(FP8X4), scales=dw_scales[:], in_=dw_grp[:].rearrange("q n t -> q (n t)")
+            )
+
+            w1_grp = prep.tile([P, E, PACK], BF16, align_bytes=64)
+            w2_grp = prep.tile([P, E, PACK], BF16, align_bytes=64)
+            ow_words = ow_raw[:].bitcast(F32)
+            for half in range(2):
+                cols = slice(half * 2 * P, (half + 1) * 2 * P)
+                w1_bank = prep_ps.tile([P, 2, 2 * P], F32, tag="words")
+                w2_bank = prep_ps.tile([P, PACK, 2 * P], BF16, tag="chunks")
+                for g in range(2):
+                    rows = 2 * half + g
+                    transpose_words(nc, w1_bank[:, :, g * P : (g + 1) * P], ow_words[:, rows, 0:WORDS], ident_f32)
+                    for c in range(CHUNKS):
+                        nc.tensor.transpose(
+                            w2_bank[:, c, g * P : (g + 1) * P],
+                            ow_raw[:, rows, E + c * P : E + (c + 1) * P],
+                            ident_bf16[:],
+                        )
+                nc.vector.tensor_copy(
+                    out=w1_grp[:, cols, :].bitcast(F32), in_=w1_bank[:].rearrange("q u n -> q n u")
+                )
+                nc.vector.tensor_copy(out=w2_grp[:, cols, :], in_=w2_bank[:].rearrange("q c n -> q n c"))
+            nc.vector.quantize_mx(
+                out=w1_codes[:].bitcast(FP8X4), scales=w1_scales[:], in_=w1_grp[:].rearrange("q n t -> q (n t)")
+            )
+            nc.vector.quantize_mx(
+                out=w2_codes[:].bitcast(FP8X4), scales=w2_scales[:], in_=w2_grp[:].rearrange("q n t -> q (n t)")
+            )
+
+        loads = ctx.enter_context(tc.tile_pool(name="loads", bufs=2))
+        work = ctx.enter_context(tc.tile_pool(name="work", bufs=2))
+        prods = ctx.enter_context(tc.tile_pool(name="prods", bufs=4))
+        stores = ctx.enter_context(tc.tile_pool(name="stores", bufs=2))
+        words_ps = ctx.enter_context(tc.psum_pool(name="words_ps", bufs=2))
+        logit_ps = ctx.enter_context(tc.psum_pool(name="logit_ps", bufs=1))
+        conv_ps = ctx.enter_context(tc.psum_pool(name="conv_ps", bufs=2))
+        out_ps = ctx.enter_context(tc.psum_pool(name="out_ps", bufs=2))
+
+        def quantise_tokens(rows_of, name):
+            bank = words_ps.tile([P, B, 2, P], F32, tag="words")
+            for b in range(B):
+                transpose_words(nc, bank[:, b, :, :], rows_of(b), ident_f32)
+            grouped = work.tile([P, B, P, PACK], BF16, align_bytes=64, tag=name + "_grp", name=name + "_grp")
+            nc.scalar.copy(out=grouped[:].bitcast(F32), in_=bank[:].rearrange("q b u n -> q b n u"))
+            codes = work.tile([P, B * P], U32, align_bytes=64, tag=name + "_codes", name=name + "_codes")
+            scales = work.tile([P, B * P], U8, align_bytes=64, tag=name + "_scales", name=name + "_scales")
+            nc.vector.quantize_mx(
+                out=codes[:].bitcast(FP8X4), scales=scales[:], in_=grouped[:].rearrange("q b n t -> q (b n t)")
+            )
+            return codes, scales
+
+        attn_sb = None
+        out_sb = None
+        for j in range(LC):
+            if j % J_ATTN == 0:
+                attn_sb = loads.tile([P, J_ATTN, B, E], BF16, tag="attn", name="attn_sb")
+                nc.sync.dma_start(out=attn_sb[:], in_=attn_rows[:, j : j + J_ATTN, :, :])
+            if j % J_OUT == 0:
+                out_sb = stores.tile([P, J_OUT, B, E], F32, tag="out", name="out_sb")
+
+            v_words = v_sb[:, PAD_L + j, :, :].bitcast(F32)
+            attn_words = attn_sb[:, j % J_ATTN, :, :].bitcast(F32)
+            v_codes, v_scales = quantise_tokens(lambda b: v_words[:, b, :], "v")
+            a_codes, a_scales = quantise_tokens(lambda b: attn_words[:, b, :], "a")
+
+            logits = logit_ps.tile([P, B, H * K], F32, tag="logits")
+            for b in range(B):
+                tokens = slice(b * P, (b + 1) * P)
+                nc.tensor.matmul_mx(
+                    out=logits[:, b, :],
+                    lhsT=v_codes[:, tokens].bitcast(FP8X4),
+                    lhsT_scale=v_scales[:, tokens],
+                    rhs=dw_codes[:].bitcast(FP8X4),
+                    rhs_scale=dw_scales[:],
+                    start=True,
+                    stop=True,
+                )
+            taps = work.tile([P, B, H, K], F32, tag="taps")
+            taps_flat = taps[:].rearrange("p b h k -> p b (h k)")
+            taps_heads = taps[:].rearrange("p b h k -> p (b h) k")
+            nc.vector.tensor_tensor(
+                out=taps_flat, in0=logits[:], in1=dyn_bias[:].unsqueeze(1).to_broadcast([P, B, H * K]), op=ALU.add
+            )
+            top = work.tile([P, B * H], F32, tag="top")
+            nc.vector.tensor_reduce(out=top[:], in_=taps_heads, axis=AXIS_X, op=ALU.max)
+            nc.vector.tensor_tensor(
+                out=taps_heads, in0=taps_heads, in1=top[:].unsqueeze(2).to_broadcast([P, B * H, K]), op=ALU.subtract
+            )
+            nc.scalar.activation(out=taps_flat, in_=taps_flat, func=ACT.Exp)
+            total = work.tile([P, B * H], F32, tag="total")
+            nc.vector.tensor_reduce(out=total[:], in_=taps_heads, axis=AXIS_X, op=ALU.add)
+            inverse = work.tile([P, B * H], F32, tag="inverse")
+            nc.vector.reciprocal(out=inverse[:], in_=total[:])
+            nc.vector.tensor_tensor(
+                out=taps_heads, in0=taps_heads, in1=inverse[:].unsqueeze(2).to_broadcast([P, B * H, K]), op=ALU.mult
+            )
+
+            conv_grp = work.tile([P, B, P, PACK], BF16, align_bytes=64, tag="conv_grp")
+            for b in range(B):
+                conv_t = conv_ps.tile([P, CHUNKS, P], F32, tag="conv_t")
+                for c in range(CHUNKS):
+                    heads = slice(c * HEADS_PER_CHUNK, (c + 1) * HEADS_PER_CHUNK)
+                    prod = prods.tile([P, K, P], F32, tag="prod")
+                    nc.vector.tensor_tensor(
+                        out=prod[:].rearrange("p k (h r) -> p k h r", r=R),
+                        in0=v_sb[:, j : j + K, b, c * P : (c + 1) * P].rearrange("p k (h r) -> p k h r", r=R),
+                        in1=taps[:, b, heads, :]
+                        .rearrange("p h k -> p k h")
+                        .unsqueeze(3)
+                        .to_broadcast([P, K, HEADS_PER_CHUNK, R]),
+                        op=ALU.mult,
+                    )
+                    for k in range(K):
+                        nc.tensor.matmul(
+                            out=conv_t[:, c, :],
+                            lhsT=prod[:, k, :],
+                            rhs=ident_f32[:],
+                            is_transpose=True,
+                            start=(k == 0),
+                            stop=(k == K - 1),
+                        )
+                nc.scalar.copy(out=conv_grp[:, b, :, :], in_=conv_t[:].rearrange("q c n -> q n c"))
+            c_codes = work.tile([P, B * P], U32, align_bytes=64, tag="c_codes")
+            c_scales = work.tile([P, B * P], U8, align_bytes=64, tag="c_scales")
+            nc.vector.quantize_mx(
+                out=c_codes[:].bitcast(FP8X4), scales=c_scales[:], in_=conv_grp[:].rearrange("q b n t -> q (b n t)")
+            )
+
+            for b in range(B):
+                tokens = slice(b * P, (b + 1) * P)
+                acc = out_ps.tile([P, E], F32, tag="acc")
+                nc.tensor.matmul_mx(
+                    out=acc[:],
+                    lhsT=a_codes[:, tokens].bitcast(FP8X4),
+                    lhsT_scale=a_scales[:, tokens],
+                    rhs=w1_codes[:].bitcast(FP8X4),
+                    rhs_scale=w1_scales[:],
+                    start=True,
+                    stop=False,
+                )
+                nc.tensor.matmul_mx(
+                    out=acc[:],
+                    lhsT=c_codes[:, tokens].bitcast(FP8X4),
+                    lhsT_scale=c_scales[:, tokens],
+                    rhs=w2_codes[:].bitcast(FP8X4),
+                    rhs_scale=w2_scales[:],
+                    start=False,
+                    stop=True,
+                )
+                nc.vector.tensor_tensor(out=out_sb[:, j % J_OUT, b, :], in0=acc[:], in1=out_bias[:], op=ALU.add)
+            if j % J_OUT == J_OUT - 1:
+                nc.sync.dma_start(out=out_rows[:, j - J_OUT + 1 : j + 1, :, :], in_=out_sb[:])

@@ -26,6 +26,7 @@ WORDS = E // 2
 J_ATTN = 4
 J_OUT = 2
 V_ROWS = 8
+SCALAR_CHUNKS = (3,)
 
 FLOPS = 2 * T * B * (E * H * K + 2 * E * E + E * K)
 
@@ -194,15 +195,26 @@ def tile_multiheadattention820_pa_t_kernel(tc, v, attn_out, dyn_w, dyn_b, out_pr
                 for c in range(CHUNKS):
                     heads = slice(c * HEADS_PER_CHUNK, (c + 1) * HEADS_PER_CHUNK)
                     prod = prods.tile([P, K, P], F32, tag="prod")
-                    nc.vector.tensor_tensor(
-                        out=prod[:].rearrange("p k (h r) -> p k h r", r=R),
-                        in0=v_sb[:, j : j + K, b, c * P : (c + 1) * P].rearrange("p k (h r) -> p k h r", r=R),
-                        in1=taps[:, b, heads, :]
-                        .rearrange("p h k -> p k h")
-                        .unsqueeze(3)
-                        .to_broadcast([P, K, HEADS_PER_CHUNK, R]),
-                        op=ALU.mult,
-                    )
+                    if c in SCALAR_CHUNKS:
+                        for h in range(HEADS_PER_CHUNK):
+                            head = c * HEADS_PER_CHUNK + h
+                            for k in range(K):
+                                nc.scalar.activation(
+                                    out=prod[:, k, h * R : (h + 1) * R],
+                                    in_=v_sb[:, j + k, b, head * R : (head + 1) * R],
+                                    func=ACT.Copy,
+                                    scale=taps[:, b, head, k : k + 1],
+                                )
+                    else:
+                        nc.vector.tensor_tensor(
+                            out=prod[:].rearrange("p k (h r) -> p k h r", r=R),
+                            in0=v_sb[:, j : j + K, b, c * P : (c + 1) * P].rearrange("p k (h r) -> p k h r", r=R),
+                            in1=taps[:, b, heads, :]
+                            .rearrange("p h k -> p k h")
+                            .unsqueeze(3)
+                            .to_broadcast([P, K, HEADS_PER_CHUNK, R]),
+                            op=ALU.mult,
+                        )
                     for k in range(K):
                         nc.tensor.matmul(
                             out=conv_t[:, c, :],

@@ -23,10 +23,11 @@ WIN = LC + K - 1
 CHUNKS = E // P
 HEADS_PER_CHUNK = P // R
 WORDS = E // 2
-J_ATTN = 4
-J_OUT = 2
+J_ATTN = 2
 V_ROWS = 8
-SCALAR_CHUNKS = (3,)
+VECTOR_CHUNKS = (0, 1)
+GPSIMD_CHUNK = 2
+SCALAR_CHUNK = 3
 
 FLOPS = 2 * T * B * (E * H * K + 2 * E * E + E * K)
 
@@ -49,24 +50,6 @@ def tile_multiheadattention820_pa_t_kernel(tc, v, attn_out, dyn_w, dyn_b, out_pr
         nc.gpsimd.memset(v_sb[0:1, 0:PAD_L, :, :], 0.0)
         nc.gpsimd.memset(v_sb[96:P, PAD_L + LC : WIN, :, :], 0.0)
 
-        dw_raw = keep.tile([P, 2, E], BF16)
-        nc.sync.dma_start(out=dw_raw[:], in_=dyn_w.rearrange("(g p) e -> p g e", p=P))
-        nc.sync.dma_start(out=v_sb[1:113, 0:PAD_L, :, :], in_=v_rows[0:112, LC - PAD_L : LC, :, :])
-        nc.sync.dma_start(out=v_sb[113:P, 0:PAD_L, :, :], in_=v_rows[112 : P - 1, LC - PAD_L : LC, :, :])
-        nc.sync.dma_start(out=v_sb[:, PAD_L : PAD_L + V_ROWS, :, :], in_=v_rows[:, 0:V_ROWS, :, :])
-        db_raw = keep.tile([P, H * K], BF16)
-        nc.sync.dma_start(out=db_raw[:], in_=dyn_b.partition_broadcast(P))
-        ow_raw = keep.tile([P, CHUNKS, 2 * E], BF16)
-        nc.sync.dma_start(out=ow_raw[:], in_=out_proj_w.rearrange("(g p) k -> p g k", p=P))
-        ob_raw = keep.tile([P, E], BF16)
-        nc.sync.dma_start(out=ob_raw[:], in_=out_proj_b.partition_broadcast(P))
-        for l0 in range(V_ROWS, LC, V_ROWS):
-            nc.sync.dma_start(
-                out=v_sb[:, PAD_L + l0 : PAD_L + l0 + V_ROWS, :, :], in_=v_rows[:, l0 : l0 + V_ROWS, :, :]
-            )
-        nc.sync.dma_start(out=v_sb[0:112, PAD_L + LC : WIN, :, :], in_=v_rows[1:113, 0:PAD_R, :, :])
-        nc.sync.dma_start(out=v_sb[112 : P - 1, PAD_L + LC : WIN, :, :], in_=v_rows[113:P, 0:PAD_R, :, :])
-
         ident_f32 = keep.tile([P, P], F32)
         make_identity(nc, ident_f32[:])
         ident_bf16 = keep.tile([P, P], BF16)
@@ -80,10 +63,29 @@ def tile_multiheadattention820_pa_t_kernel(tc, v, attn_out, dyn_w, dyn_b, out_pr
         w2_scales = keep.tile([P, E], U8, align_bytes=64)
         dyn_bias = keep.tile([P, H * K], F32)
         out_bias = keep.tile([P, E], F32)
-        nc.vector.tensor_copy(out=dyn_bias[:], in_=db_raw[:])
-        nc.vector.tensor_copy(out=out_bias[:], in_=ob_raw[:])
 
         with tc.tile_pool(name="prep", bufs=1) as prep, tc.psum_pool(name="prep_ps", bufs=2) as prep_ps:
+            dw_raw = prep.tile([P, 2, E], BF16)
+            nc.sync.dma_start(out=dw_raw[:], in_=dyn_w.rearrange("(g p) e -> p g e", p=P))
+            nc.sync.dma_start(out=v_sb[1:113, 0:PAD_L, :, :], in_=v_rows[0:112, LC - PAD_L : LC, :, :])
+            nc.sync.dma_start(out=v_sb[113:P, 0:PAD_L, :, :], in_=v_rows[112 : P - 1, LC - PAD_L : LC, :, :])
+            nc.sync.dma_start(out=v_sb[:, PAD_L : PAD_L + V_ROWS, :, :], in_=v_rows[:, 0:V_ROWS, :, :])
+            db_raw = prep.tile([P, H * K], BF16)
+            nc.sync.dma_start(out=db_raw[:], in_=dyn_b.partition_broadcast(P))
+            ow_raw = prep.tile([P, CHUNKS, 2 * E], BF16)
+            nc.sync.dma_start(out=ow_raw[:], in_=out_proj_w.rearrange("(g p) k -> p g k", p=P))
+            ob_raw = prep.tile([P, E], BF16)
+            nc.sync.dma_start(out=ob_raw[:], in_=out_proj_b.partition_broadcast(P))
+            for l0 in range(V_ROWS, LC, V_ROWS):
+                nc.sync.dma_start(
+                    out=v_sb[:, PAD_L + l0 : PAD_L + l0 + V_ROWS, :, :], in_=v_rows[:, l0 : l0 + V_ROWS, :, :]
+                )
+            nc.sync.dma_start(out=v_sb[0:112, PAD_L + LC : WIN, :, :], in_=v_rows[1:113, 0:PAD_R, :, :])
+            nc.sync.dma_start(out=v_sb[112 : P - 1, PAD_L + LC : WIN, :, :], in_=v_rows[113:P, 0:PAD_R, :, :])
+
+            nc.vector.tensor_copy(out=dyn_bias[:], in_=db_raw[:])
+            nc.vector.tensor_copy(out=out_bias[:], in_=ob_raw[:])
+
             dw_grp = prep.tile([P, H * K, PACK], BF16, align_bytes=64)
             dw_words = dw_raw[:].bitcast(F32)
             dw_bank = prep_ps.tile([P, 2, 2 * P], F32, tag="words")
@@ -123,12 +125,13 @@ def tile_multiheadattention820_pa_t_kernel(tc, v, attn_out, dyn_w, dyn_b, out_pr
 
         loads = ctx.enter_context(tc.tile_pool(name="loads", bufs=2))
         work = ctx.enter_context(tc.tile_pool(name="work", bufs=2))
-        prods = ctx.enter_context(tc.tile_pool(name="prods", bufs=4))
+        prods = ctx.enter_context(tc.tile_pool(name="prods", bufs=2))
         stores = ctx.enter_context(tc.tile_pool(name="stores", bufs=2))
         words_ps = ctx.enter_context(tc.psum_pool(name="words_ps", bufs=2))
         logit_ps = ctx.enter_context(tc.psum_pool(name="logit_ps", bufs=1))
+        taps_ps = ctx.enter_context(tc.psum_pool(name="taps_ps", bufs=2))
         conv_ps = ctx.enter_context(tc.psum_pool(name="conv_ps", bufs=2))
-        out_ps = ctx.enter_context(tc.psum_pool(name="out_ps", bufs=2))
+        out_ps = ctx.enter_context(tc.psum_pool(name="out_ps", bufs=1))
 
         def quantise_tokens(rows_of, name):
             bank = words_ps.tile([P, B, 2, P], F32, tag="words")
@@ -143,15 +146,7 @@ def tile_multiheadattention820_pa_t_kernel(tc, v, attn_out, dyn_w, dyn_b, out_pr
             )
             return codes, scales
 
-        attn_sb = None
-        out_sb = None
-        for j in range(LC):
-            if j % J_ATTN == 0:
-                attn_sb = loads.tile([P, J_ATTN, B, E], BF16, tag="attn", name="attn_sb")
-                nc.sync.dma_start(out=attn_sb[:], in_=attn_rows[:, j : j + J_ATTN, :, :])
-            if j % J_OUT == 0:
-                out_sb = stores.tile([P, J_OUT, B, E], F32, tag="out", name="out_sb")
-
+        def taps_of_step(j, attn_sb):
             v_words = v_sb[:, PAD_L + j, :, :].bitcast(F32)
             attn_words = attn_sb[:, j % J_ATTN, :, :].bitcast(F32)
             v_codes, v_scales = quantise_tokens(lambda b: v_words[:, b, :], "v")
@@ -188,41 +183,65 @@ def tile_multiheadattention820_pa_t_kernel(tc, v, attn_out, dyn_w, dyn_b, out_pr
             nc.vector.tensor_tensor(
                 out=taps_heads, in0=taps_heads, in1=inverse[:].unsqueeze(2).to_broadcast([P, B * H, K]), op=ALU.mult
             )
+            taps_cols = taps[:].rearrange("p b h k -> p (b h k)")
+            flipped_bank = words_ps.tile([P, PACK, P], F32, tag="words")
+            for q in range(PACK):
+                nc.tensor.transpose(flipped_bank[:, q, :], taps_cols[:, q * P : (q + 1) * P], ident_f32[:])
+            flipped = work.tile([P, PACK, P], F32, tag="flipped")
+            nc.scalar.copy(out=flipped[:], in_=flipped_bank[:])
+            taps_bank = taps_ps.tile([P, B, H, K], F32, tag="taps_bank")
+            bank_cols = taps_bank[:].rearrange("p b h k -> p (b h k)")
+            for q in range(PACK):
+                nc.tensor.transpose(bank_cols[:, q * P : (q + 1) * P], flipped[:, q, :], ident_f32[:])
+            return a_codes, a_scales, taps, taps_bank
 
+        def spread(taps_of_heads):
+            return taps_of_heads.rearrange("p h k -> p k h").unsqueeze(3).to_broadcast([P, K, HEADS_PER_CHUNK, R])
+
+        def convolve_and_project(j, a_codes, a_scales, taps, taps_bank):
             conv_grp = work.tile([P, B, P, PACK], BF16, align_bytes=64, tag="conv_grp")
             for b in range(B):
-                conv_t = conv_ps.tile([P, CHUNKS, P], F32, tag="conv_t")
+                prod = [prods.tile([P, K, P], F32, tag="prod%d" % c, name="prod%d" % c) for c in range(CHUNKS)]
                 for c in range(CHUNKS):
                     heads = slice(c * HEADS_PER_CHUNK, (c + 1) * HEADS_PER_CHUNK)
-                    prod = prods.tile([P, K, P], F32, tag="prod")
-                    if c in SCALAR_CHUNKS:
+                    window = v_sb[:, j : j + K, b, c * P : (c + 1) * P].rearrange("p k (h r) -> p k h r", r=R)
+                    target = prod[c][:].rearrange("p k (h r) -> p k h r", r=R)
+                    if c in VECTOR_CHUNKS:
+                        nc.vector.tensor_tensor(out=target, in0=window, in1=spread(taps_bank[:, b, heads, :]), op=ALU.mult)
+                    elif c == GPSIMD_CHUNK:
+                        nc.gpsimd.tensor_tensor(out=target, in0=window, in1=spread(taps[:, b, heads, :]), op=ALU.mult)
+                    else:
                         for h in range(HEADS_PER_CHUNK):
                             head = c * HEADS_PER_CHUNK + h
                             for k in range(K):
                                 nc.scalar.activation(
-                                    out=prod[:, k, h * R : (h + 1) * R],
+                                    out=prod[c][:, k, h * R : (h + 1) * R],
                                     in_=v_sb[:, j + k, b, head * R : (head + 1) * R],
                                     func=ACT.Copy,
                                     scale=taps[:, b, head, k : k + 1],
                                 )
-                    else:
-                        nc.vector.tensor_tensor(
-                            out=prod[:].rearrange("p k (h r) -> p k h r", r=R),
-                            in0=v_sb[:, j : j + K, b, c * P : (c + 1) * P].rearrange("p k (h r) -> p k h r", r=R),
-                            in1=taps[:, b, heads, :]
-                            .rearrange("p h k -> p k h")
-                            .unsqueeze(3)
-                            .to_broadcast([P, K, HEADS_PER_CHUNK, R]),
-                            op=ALU.mult,
+                left = {}
+                for c in range(CHUNKS):
+                    left[c] = K
+                    if c in VECTOR_CHUNKS or c == GPSIMD_CHUNK:
+                        engine = nc.vector if c in VECTOR_CHUNKS else nc.gpsimd
+                        left[c] = K // 2
+                        engine.tensor_tensor(
+                            out=prod[c][:, 0 : K // 2, :],
+                            in0=prod[c][:, 0 : K // 2, :],
+                            in1=prod[c][:, K // 2 : K, :],
+                            op=ALU.add,
                         )
-                    for k in range(K):
+                conv_t = conv_ps.tile([P, CHUNKS, P], F32, tag="conv_t")
+                for c in range(CHUNKS):
+                    for k in range(left[c]):
                         nc.tensor.matmul(
                             out=conv_t[:, c, :],
-                            lhsT=prod[:, k, :],
+                            lhsT=prod[c][:, k, :],
                             rhs=ident_f32[:],
                             is_transpose=True,
                             start=(k == 0),
-                            stop=(k == K - 1),
+                            stop=(k == left[c] - 1),
                         )
                 nc.scalar.copy(out=conv_grp[:, b, :, :], in_=conv_t[:].rearrange("q c n -> q n c"))
             c_codes = work.tile([P, B * P], U32, align_bytes=64, tag="c_codes")
@@ -231,6 +250,7 @@ def tile_multiheadattention820_pa_t_kernel(tc, v, attn_out, dyn_w, dyn_b, out_pr
                 out=c_codes[:].bitcast(FP8X4), scales=c_scales[:], in_=conv_grp[:].rearrange("q b n t -> q (b n t)")
             )
 
+            out_sb = stores.tile([P, B, E], F32, tag="out")
             for b in range(B):
                 tokens = slice(b * P, (b + 1) * P)
                 acc = out_ps.tile([P, E], F32, tag="acc")
@@ -252,6 +272,21 @@ def tile_multiheadattention820_pa_t_kernel(tc, v, attn_out, dyn_w, dyn_b, out_pr
                     start=False,
                     stop=True,
                 )
-                nc.vector.tensor_tensor(out=out_sb[:, j % J_OUT, b, :], in0=acc[:], in1=out_bias[:], op=ALU.add)
-            if j % J_OUT == J_OUT - 1:
-                nc.sync.dma_start(out=out_rows[:, j - J_OUT + 1 : j + 1, :, :], in_=out_sb[:])
+                nc.vector.tensor_tensor(out=out_sb[:, b, :], in0=acc[:], in1=out_bias[:], op=ALU.add)
+            nc.sync.dma_start(out=out_rows[:, j, :, :], in_=out_sb[:])
+
+        def load_attn(j):
+            attn_sb = loads.tile([P, J_ATTN, B, E], BF16, tag="attn", name="attn_sb")
+            nc.sync.dma_start(out=attn_sb[:], in_=attn_rows[:, j : j + J_ATTN, :, :])
+            return attn_sb
+
+        attn_sb = load_attn(0)
+        ready = taps_of_step(0, attn_sb)
+        for j in range(LC):
+            following = None
+            if j + 1 < LC:
+                if (j + 1) % J_ATTN == 0:
+                    attn_sb = load_attn(j + 1)
+                following = taps_of_step(j + 1, attn_sb)
+            convolve_and_project(j, *ready)
+            ready = following

@@ -25,9 +25,8 @@ HEADS_PER_CHUNK = P // R
 WORDS = E // 2
 J_ATTN = 2
 V_ROWS = 8
-VECTOR_CHUNKS = (0, 1)
-GPSIMD_CHUNK = 2
-SCALAR_CHUNK = 3
+SCALAR_CHUNKS = (0, 3)
+VECTOR_CHUNKS = (1, 2)
 
 FLOPS = 2 * T * B * (E * H * K + 2 * E * E + E * K)
 
@@ -126,138 +125,178 @@ def tile_multiheadattention820_pa_t_kernel(tc, v, attn_out, dyn_w, dyn_b, out_pr
         loads = ctx.enter_context(tc.tile_pool(name="loads", bufs=2))
         work = ctx.enter_context(tc.tile_pool(name="work", bufs=2))
         prods = ctx.enter_context(tc.tile_pool(name="prods", bufs=2))
-        stores = ctx.enter_context(tc.tile_pool(name="stores", bufs=2))
-        words_ps = ctx.enter_context(tc.psum_pool(name="words_ps", bufs=2))
+        words_ps = ctx.enter_context(tc.psum_pool(name="words_ps", bufs=1))
         logit_ps = ctx.enter_context(tc.psum_pool(name="logit_ps", bufs=1))
-        taps_ps = ctx.enter_context(tc.psum_pool(name="taps_ps", bufs=2))
-        conv_ps = ctx.enter_context(tc.psum_pool(name="conv_ps", bufs=2))
+        conv_ps = ctx.enter_context(tc.psum_pool(name="conv_ps", bufs=3))
         out_ps = ctx.enter_context(tc.psum_pool(name="out_ps", bufs=1))
 
-        def quantise_tokens(rows_of, name):
-            bank = words_ps.tile([P, B, 2, P], F32, tag="words")
-            for b in range(B):
-                transpose_words(nc, bank[:, b, :, :], rows_of(b), ident_f32)
-            grouped = work.tile([P, B, P, PACK], BF16, align_bytes=64, tag=name + "_grp", name=name + "_grp")
-            nc.scalar.copy(out=grouped[:].bitcast(F32), in_=bank[:].rearrange("q b u n -> q b n u"))
-            codes = work.tile([P, B * P], U32, align_bytes=64, tag=name + "_codes", name=name + "_codes")
-            scales = work.tile([P, B * P], U8, align_bytes=64, tag=name + "_scales", name=name + "_scales")
-            nc.vector.quantize_mx(
-                out=codes[:].bitcast(FP8X4), scales=scales[:], in_=grouped[:].rearrange("q b n t -> q (b n t)")
-            )
-            return codes, scales
+        attn_tiles = {}
+        step = {}
+        half = {}
 
-        def taps_of_step(j, attn_sb):
-            v_words = v_sb[:, PAD_L + j, :, :].bitcast(F32)
-            attn_words = attn_sb[:, j % J_ATTN, :, :].bitcast(F32)
-            v_codes, v_scales = quantise_tokens(lambda b: v_words[:, b, :], "v")
-            a_codes, a_scales = quantise_tokens(lambda b: attn_words[:, b, :], "a")
+        def load_attn(j):
+            attn_tiles[j] = loads.tile([P, J_ATTN, B, E], BF16, tag="attn", name="attn_sb")
+            nc.sync.dma_start(out=attn_tiles[j][:], in_=attn_rows[:, j : j + J_ATTN, :, :])
 
+        def flip_inputs(j):
+            attn_sb = attn_tiles[j - j % J_ATTN]
+            rows = {"v": v_sb[:, PAD_L + j, :, :].bitcast(F32), "a": attn_sb[:, j % J_ATTN, :, :].bitcast(F32)}
+            step[j] = {}
+            for name in ("v", "a"):
+                bank = words_ps.tile([P, B, 2, P], F32, tag=name + "_bank", name=name + "_bank")
+                for b in range(B):
+                    transpose_words(nc, bank[:, b, :, :], rows[name][:, b, :], ident_f32)
+                step[j][name + "_bank"] = bank
+
+        def group_inputs(j):
+            for name in ("v", "a"):
+                grouped = work.tile([P, B, P, PACK], BF16, align_bytes=64, tag=name + "_grp", name=name + "_grp")
+                nc.scalar.copy(
+                    out=grouped[:].bitcast(F32), in_=step[j][name + "_bank"][:].rearrange("q b u n -> q b n u")
+                )
+                step[j][name + "_grp"] = grouped
+
+        def quantise_inputs(j):
+            for name in ("v", "a"):
+                slots = 2 if name == "v" else 4
+                codes = work.tile(
+                    [P, B * P], U32, align_bytes=64, tag=name + "_codes", name=name + "_codes", bufs=slots
+                )
+                scales = work.tile(
+                    [P, B * P], U8, align_bytes=64, tag=name + "_scales", name=name + "_scales", bufs=slots
+                )
+                nc.vector.quantize_mx(
+                    out=codes[:].bitcast(FP8X4),
+                    scales=scales[:],
+                    in_=step[j][name + "_grp"][:].rearrange("q b n t -> q (b n t)"),
+                )
+                step[j][name + "_codes"] = codes
+                step[j][name + "_scales"] = scales
+
+        def logits_of(j):
             logits = logit_ps.tile([P, B, H * K], F32, tag="logits")
             for b in range(B):
                 tokens = slice(b * P, (b + 1) * P)
                 nc.tensor.matmul_mx(
                     out=logits[:, b, :],
-                    lhsT=v_codes[:, tokens].bitcast(FP8X4),
-                    lhsT_scale=v_scales[:, tokens],
+                    lhsT=step[j]["v_codes"][:, tokens].bitcast(FP8X4),
+                    lhsT_scale=step[j]["v_scales"][:, tokens],
                     rhs=dw_codes[:].bitcast(FP8X4),
                     rhs_scale=dw_scales[:],
                     start=True,
                     stop=True,
                 )
+            step[j]["logits"] = logits
+
+        def by_head(taps):
+            return taps[:].rearrange("p b h k -> p (b h) k")
+
+        def shift_logits(j):
             taps = work.tile([P, B, H, K], F32, tag="taps")
-            taps_flat = taps[:].rearrange("p b h k -> p b (h k)")
-            taps_heads = taps[:].rearrange("p b h k -> p (b h) k")
             nc.vector.tensor_tensor(
-                out=taps_flat, in0=logits[:], in1=dyn_bias[:].unsqueeze(1).to_broadcast([P, B, H * K]), op=ALU.add
+                out=taps[:].rearrange("p b h k -> p b (h k)"),
+                in0=step[j]["logits"][:],
+                in1=dyn_bias[:].unsqueeze(1).to_broadcast([P, B, H * K]),
+                op=ALU.add,
             )
             top = work.tile([P, B * H], F32, tag="top")
-            nc.vector.tensor_reduce(out=top[:], in_=taps_heads, axis=AXIS_X, op=ALU.max)
+            nc.vector.tensor_reduce(out=top[:], in_=by_head(taps), axis=AXIS_X, op=ALU.max)
             nc.vector.tensor_tensor(
-                out=taps_heads, in0=taps_heads, in1=top[:].unsqueeze(2).to_broadcast([P, B * H, K]), op=ALU.subtract
+                out=by_head(taps), in0=by_head(taps), in1=top[:].unsqueeze(2).to_broadcast([P, B * H, K]), op=ALU.subtract
             )
-            nc.scalar.activation(out=taps_flat, in_=taps_flat, func=ACT.Exp)
+            step[j]["taps"] = taps
+
+        def exponentials(j):
+            flat = step[j]["taps"][:].rearrange("p b h k -> p (b h k)")
+            nc.scalar.activation(out=flat, in_=flat, func=ACT.Exp)
+
+        def normalise(j):
+            taps = step[j]["taps"]
             total = work.tile([P, B * H], F32, tag="total")
-            nc.vector.tensor_reduce(out=total[:], in_=taps_heads, axis=AXIS_X, op=ALU.add)
+            nc.vector.tensor_reduce(out=total[:], in_=by_head(taps), axis=AXIS_X, op=ALU.add)
             inverse = work.tile([P, B * H], F32, tag="inverse")
             nc.vector.reciprocal(out=inverse[:], in_=total[:])
             nc.vector.tensor_tensor(
-                out=taps_heads, in0=taps_heads, in1=inverse[:].unsqueeze(2).to_broadcast([P, B * H, K]), op=ALU.mult
+                out=by_head(taps), in0=by_head(taps), in1=inverse[:].unsqueeze(2).to_broadcast([P, B * H, K]), op=ALU.mult
             )
-            taps_cols = taps[:].rearrange("p b h k -> p (b h k)")
-            flipped_bank = words_ps.tile([P, PACK, P], F32, tag="words")
-            for q in range(PACK):
-                nc.tensor.transpose(flipped_bank[:, q, :], taps_cols[:, q * P : (q + 1) * P], ident_f32[:])
-            flipped = work.tile([P, PACK, P], F32, tag="flipped")
-            nc.scalar.copy(out=flipped[:], in_=flipped_bank[:])
-            taps_bank = taps_ps.tile([P, B, H, K], F32, tag="taps_bank")
-            bank_cols = taps_bank[:].rearrange("p b h k -> p (b h k)")
-            for q in range(PACK):
-                nc.tensor.transpose(bank_cols[:, q * P : (q + 1) * P], flipped[:, q, :], ident_f32[:])
-            return a_codes, a_scales, taps, taps_bank
 
-        def spread(taps_of_heads):
-            return taps_of_heads.rearrange("p h k -> p k h").unsqueeze(3).to_broadcast([P, K, HEADS_PER_CHUNK, R])
+        def new_products(x, c):
+            prod = prods.tile([P, K, P], F32, tag="prod%d" % c, name="prod%d" % c)
+            half[x][c] = prod
+            return prod
 
-        def convolve_and_project(j, a_codes, a_scales, taps, taps_bank):
-            conv_grp = work.tile([P, B, P, PACK], BF16, align_bytes=64, tag="conv_grp")
-            for b in range(B):
-                prod = [prods.tile([P, K, P], F32, tag="prod%d" % c, name="prod%d" % c) for c in range(CHUNKS)]
-                for c in range(CHUNKS):
-                    heads = slice(c * HEADS_PER_CHUNK, (c + 1) * HEADS_PER_CHUNK)
-                    window = v_sb[:, j : j + K, b, c * P : (c + 1) * P].rearrange("p k (h r) -> p k h r", r=R)
-                    target = prod[c][:].rearrange("p k (h r) -> p k h r", r=R)
-                    if c in VECTOR_CHUNKS:
-                        nc.vector.tensor_tensor(out=target, in0=window, in1=spread(taps_bank[:, b, heads, :]), op=ALU.mult)
-                    elif c == GPSIMD_CHUNK:
-                        nc.gpsimd.tensor_tensor(out=target, in0=window, in1=spread(taps[:, b, heads, :]), op=ALU.mult)
-                    else:
-                        for h in range(HEADS_PER_CHUNK):
-                            head = c * HEADS_PER_CHUNK + h
-                            for k in range(K):
-                                nc.scalar.activation(
-                                    out=prod[c][:, k, h * R : (h + 1) * R],
-                                    in_=v_sb[:, j + k, b, head * R : (head + 1) * R],
-                                    func=ACT.Copy,
-                                    scale=taps[:, b, head, k : k + 1],
-                                )
-                left = {}
-                for c in range(CHUNKS):
-                    left[c] = K
-                    if c in VECTOR_CHUNKS or c == GPSIMD_CHUNK:
-                        engine = nc.vector if c in VECTOR_CHUNKS else nc.gpsimd
-                        left[c] = K // 2
-                        engine.tensor_tensor(
-                            out=prod[c][:, 0 : K // 2, :],
-                            in0=prod[c][:, 0 : K // 2, :],
-                            in1=prod[c][:, K // 2 : K, :],
-                            op=ALU.add,
-                        )
-                conv_t = conv_ps.tile([P, CHUNKS, P], F32, tag="conv_t")
-                for c in range(CHUNKS):
-                    for k in range(left[c]):
-                        nc.tensor.matmul(
-                            out=conv_t[:, c, :],
-                            lhsT=prod[c][:, k, :],
-                            rhs=ident_f32[:],
-                            is_transpose=True,
-                            start=(k == 0),
-                            stop=(k == left[c] - 1),
-                        )
-                nc.scalar.copy(out=conv_grp[:, b, :, :], in_=conv_t[:].rearrange("q c n -> q n c"))
+        def scalar_products(x, c):
+            j, b = divmod(x, B)
+            prod = new_products(x, c)
+            for h in range(HEADS_PER_CHUNK):
+                head = c * HEADS_PER_CHUNK + h
+                for k in range(K):
+                    nc.scalar.activation(
+                        out=prod[:, k, h * R : (h + 1) * R],
+                        in_=v_sb[:, j + k, b, head * R : (head + 1) * R],
+                        func=ACT.Copy,
+                        scale=step[j]["taps"][:, b, head, k : k + 1],
+                    )
+
+        def vector_products(x, c):
+            j, b = divmod(x, B)
+            prod = new_products(x, c)
+            heads = slice(c * HEADS_PER_CHUNK, (c + 1) * HEADS_PER_CHUNK)
+            nc.vector.tensor_tensor(
+                out=prod[:].rearrange("p k (h r) -> p k h r", r=R),
+                in0=v_sb[:, j : j + K, b, c * P : (c + 1) * P].rearrange("p k (h r) -> p k h r", r=R),
+                in1=step[j]["taps"][:, b, heads, :]
+                .rearrange("p h k -> p k h")
+                .unsqueeze(3)
+                .to_broadcast([P, K, HEADS_PER_CHUNK, R]),
+                op=ALU.mult,
+            )
+
+        def vector_fold(x, c):
+            prod = half[x][c]
+            nc.vector.tensor_tensor(
+                out=prod[:, 0 : K // 2, :], in0=prod[:, 0 : K // 2, :], in1=prod[:, K // 2 : K, :], op=ALU.add
+            )
+
+        def add_up(x, c):
+            if c == 0:
+                half[x]["conv_t"] = conv_ps.tile([P, CHUNKS, P], F32, tag="conv_t", name="conv_t")
+            left = K // 2 if c in VECTOR_CHUNKS else K
+            for k in range(left):
+                nc.tensor.matmul(
+                    out=half[x]["conv_t"][:, c, :],
+                    lhsT=half[x][c][:, k, :],
+                    rhs=ident_f32[:],
+                    is_transpose=True,
+                    start=(k == 0),
+                    stop=(k == left - 1),
+                )
+
+        def round_conv(x):
+            j, b = divmod(x, B)
+            if b == 0:
+                step[j]["conv_grp"] = work.tile([P, B, P, PACK], BF16, align_bytes=64, tag="conv_grp", name="conv_grp")
+            nc.scalar.copy(out=step[j]["conv_grp"][:, b, :, :], in_=half[x]["conv_t"][:].rearrange("q c n -> q n c"))
+
+        def quantise_conv(j):
             c_codes = work.tile([P, B * P], U32, align_bytes=64, tag="c_codes")
             c_scales = work.tile([P, B * P], U8, align_bytes=64, tag="c_scales")
             nc.vector.quantize_mx(
-                out=c_codes[:].bitcast(FP8X4), scales=c_scales[:], in_=conv_grp[:].rearrange("q b n t -> q (b n t)")
+                out=c_codes[:].bitcast(FP8X4),
+                scales=c_scales[:],
+                in_=step[j]["conv_grp"][:].rearrange("q b n t -> q (b n t)"),
             )
+            step[j]["c_codes"] = c_codes
+            step[j]["c_scales"] = c_scales
 
-            out_sb = stores.tile([P, B, E], F32, tag="out")
+        def project(j):
             for b in range(B):
                 tokens = slice(b * P, (b + 1) * P)
-                acc = out_ps.tile([P, E], F32, tag="acc")
+                acc = out_ps.tile([P, E], F32, tag="acc%d" % b, name="acc%d" % b)
                 nc.tensor.matmul_mx(
                     out=acc[:],
-                    lhsT=a_codes[:, tokens].bitcast(FP8X4),
-                    lhsT_scale=a_scales[:, tokens],
+                    lhsT=step[j]["a_codes"][:, tokens].bitcast(FP8X4),
+                    lhsT_scale=step[j]["a_scales"][:, tokens],
                     rhs=w1_codes[:].bitcast(FP8X4),
                     rhs_scale=w1_scales[:],
                     start=True,
@@ -265,28 +304,77 @@ def tile_multiheadattention820_pa_t_kernel(tc, v, attn_out, dyn_w, dyn_b, out_pr
                 )
                 nc.tensor.matmul_mx(
                     out=acc[:],
-                    lhsT=c_codes[:, tokens].bitcast(FP8X4),
-                    lhsT_scale=c_scales[:, tokens],
+                    lhsT=step[j]["c_codes"][:, tokens].bitcast(FP8X4),
+                    lhsT_scale=step[j]["c_scales"][:, tokens],
                     rhs=w2_codes[:].bitcast(FP8X4),
                     rhs_scale=w2_scales[:],
                     start=False,
                     stop=True,
                 )
-                nc.vector.tensor_tensor(out=out_sb[:, b, :], in0=acc[:], in1=out_bias[:], op=ALU.add)
+                step[j]["acc%d" % b] = acc
+
+        def store(j):
+            out_sb = work.tile([P, B, E], F32, tag="out_sb")
+            for b in range(B):
+                nc.vector.tensor_tensor(out=out_sb[:, b, :], in0=step[j]["acc%d" % b][:], in1=out_bias[:], op=ALU.add)
             nc.sync.dma_start(out=out_rows[:, j, :, :], in_=out_sb[:])
 
-        def load_attn(j):
-            attn_sb = loads.tile([P, J_ATTN, B, E], BF16, tag="attn", name="attn_sb")
-            nc.sync.dma_start(out=attn_sb[:], in_=attn_rows[:, j : j + J_ATTN, :, :])
-            return attn_sb
-
-        attn_sb = load_attn(0)
-        ready = taps_of_step(0, attn_sb)
-        for j in range(LC):
-            following = None
-            if j + 1 < LC:
-                if (j + 1) % J_ATTN == 0:
-                    attn_sb = load_attn(j + 1)
-                following = taps_of_step(j + 1, attn_sb)
-            convolve_and_project(j, *ready)
-            ready = following
+        HALF_STEPS = B * LC
+        load_attn(0)
+        flip_inputs(0)
+        group_inputs(0)
+        quantise_inputs(0)
+        logits_of(0)
+        shift_logits(0)
+        exponentials(0)
+        normalise(0)
+        with tc.manual_schedule():
+            for x in range(HALF_STEPS + 3):
+                j, b = divmod(x, B)
+                first, second = b == 0, b == 1
+                products = x < HALF_STEPS
+                additions = 1 <= x <= HALF_STEPS
+                taps_ahead = j + 1 < LC
+                if products:
+                    half[x] = {}
+                if first and j + J_ATTN < LC and j % J_ATTN == 0:
+                    load_attn(j + J_ATTN)
+                if first and taps_ahead:
+                    flip_inputs(j + 1)
+                if second and taps_ahead:
+                    exponentials(j + 1)
+                if products:
+                    scalar_products(x, SCALAR_CHUNKS[0])
+                if 2 <= x < HALF_STEPS + 2:
+                    round_conv(x - 2)
+                if products:
+                    vector_products(x, VECTOR_CHUNKS[0])
+                if first and taps_ahead:
+                    group_inputs(j + 1)
+                if additions:
+                    add_up(x - 1, 0)
+                    add_up(x - 1, 1)
+                if second and taps_ahead:
+                    normalise(j + 1)
+                if second and 1 <= j <= LC:
+                    quantise_conv(j - 1)
+                if products:
+                    vector_products(x, VECTOR_CHUNKS[1])
+                if first and taps_ahead:
+                    quantise_inputs(j + 1)
+                if first and 2 <= j <= LC + 1:
+                    store(j - 2)
+                if products:
+                    vector_fold(x, VECTOR_CHUNKS[0])
+                    vector_fold(x, VECTOR_CHUNKS[1])
+                    scalar_products(x, SCALAR_CHUNKS[1])
+                if additions:
+                    add_up(x - 1, 2)
+                if first and taps_ahead:
+                    logits_of(j + 1)
+                if second and 1 <= j <= LC:
+                    project(j - 1)
+                if additions:
+                    add_up(x - 1, 3)
+                if first and taps_ahead:
+                    shift_logits(j + 1)

@@ -46,13 +46,12 @@ def tile_multiheadattention820_pa_t_kernel(tc, v, attn_out, dyn_w, dyn_b, out_pr
         keep = ctx.enter_context(tc.tile_pool(name="keep", bufs=1))
 
         v_sb = keep.tile([P, WIN, B, E], BF16)
-        nc.gpsimd.memset(v_sb[0:1, 0:PAD_L, :, :], 0.0)
-        nc.gpsimd.memset(v_sb[96:P, PAD_L + LC : WIN, :, :], 0.0)
-
         ident_f32 = keep.tile([P, P], F32)
         make_identity(nc, ident_f32[:])
         ident_bf16 = keep.tile([P, P], BF16)
         make_identity(nc, ident_bf16[:])
+        nc.vector.memset(v_sb[0:1, 0:PAD_L, :, :], 0.0)
+        nc.gpsimd.memset(v_sb[96:P, PAD_L + LC : WIN, :, :], 0.0)
 
         dw_codes = keep.tile([P, H * K], U32, align_bytes=64)
         dw_scales = keep.tile([P, H * K], U8, align_bytes=64)
@@ -63,14 +62,22 @@ def tile_multiheadattention820_pa_t_kernel(tc, v, attn_out, dyn_w, dyn_b, out_pr
         dyn_bias = keep.tile([P, H * K], F32)
         out_bias = keep.tile([P, E], F32)
 
+        loads = ctx.enter_context(tc.tile_pool(name="loads", bufs=2))
+        attn_tiles = {}
+
+        def load_attn(j):
+            attn_tiles[j] = loads.tile([P, J_ATTN, B, E], BF16, tag="attn", name="attn_sb")
+            nc.sync.dma_start(out=attn_tiles[j][:], in_=attn_rows[:, j : j + J_ATTN, :, :])
+
         with tc.tile_pool(name="prep", bufs=1) as prep, tc.psum_pool(name="prep_ps", bufs=2) as prep_ps:
             dw_raw = prep.tile([P, 2, E], BF16)
             nc.sync.dma_start(out=dw_raw[:], in_=dyn_w.rearrange("(g p) e -> p g e", p=P))
-            nc.sync.dma_start(out=v_sb[1:113, 0:PAD_L, :, :], in_=v_rows[0:112, LC - PAD_L : LC, :, :])
-            nc.sync.dma_start(out=v_sb[113:P, 0:PAD_L, :, :], in_=v_rows[112 : P - 1, LC - PAD_L : LC, :, :])
             nc.sync.dma_start(out=v_sb[:, PAD_L : PAD_L + V_ROWS, :, :], in_=v_rows[:, 0:V_ROWS, :, :])
+            load_attn(0)
             db_raw = prep.tile([P, H * K], BF16)
             nc.sync.dma_start(out=db_raw[:], in_=dyn_b.partition_broadcast(P))
+            nc.sync.dma_start(out=v_sb[1:113, 0:PAD_L, :, :], in_=v_rows[0:112, LC - PAD_L : LC, :, :])
+            nc.sync.dma_start(out=v_sb[113:P, 0:PAD_L, :, :], in_=v_rows[112 : P - 1, LC - PAD_L : LC, :, :])
             ow_raw = prep.tile([P, CHUNKS, 2 * E], BF16)
             nc.sync.dma_start(out=ow_raw[:], in_=out_proj_w.rearrange("(g p) k -> p g k", p=P))
             ob_raw = prep.tile([P, E], BF16)
@@ -122,7 +129,6 @@ def tile_multiheadattention820_pa_t_kernel(tc, v, attn_out, dyn_w, dyn_b, out_pr
                 out=w2_codes[:].bitcast(FP8X4), scales=w2_scales[:], in_=w2_grp[:].rearrange("q n t -> q (n t)")
             )
 
-        loads = ctx.enter_context(tc.tile_pool(name="loads", bufs=2))
         work = ctx.enter_context(tc.tile_pool(name="work", bufs=2))
         prods = ctx.enter_context(tc.tile_pool(name="prods", bufs=2))
         words_ps = ctx.enter_context(tc.psum_pool(name="words_ps", bufs=1))
@@ -130,13 +136,8 @@ def tile_multiheadattention820_pa_t_kernel(tc, v, attn_out, dyn_w, dyn_b, out_pr
         conv_ps = ctx.enter_context(tc.psum_pool(name="conv_ps", bufs=3))
         out_ps = ctx.enter_context(tc.psum_pool(name="out_ps", bufs=1))
 
-        attn_tiles = {}
         step = {}
         half = {}
-
-        def load_attn(j):
-            attn_tiles[j] = loads.tile([P, J_ATTN, B, E], BF16, tag="attn", name="attn_sb")
-            nc.sync.dma_start(out=attn_tiles[j][:], in_=attn_rows[:, j : j + J_ATTN, :, :])
 
         def flip_inputs(j):
             attn_sb = attn_tiles[j - j % J_ATTN]
@@ -320,7 +321,6 @@ def tile_multiheadattention820_pa_t_kernel(tc, v, attn_out, dyn_w, dyn_b, out_pr
             nc.sync.dma_start(out=out_rows[:, j, :, :], in_=out_sb[:])
 
         HALF_STEPS = B * LC
-        load_attn(0)
         flip_inputs(0)
         group_inputs(0)
         quantise_inputs(0)
@@ -343,11 +343,10 @@ def tile_multiheadattention820_pa_t_kernel(tc, v, attn_out, dyn_w, dyn_b, out_pr
                     flip_inputs(j + 1)
                 if second and taps_ahead:
                     exponentials(j + 1)
-                if products:
-                    scalar_products(x, SCALAR_CHUNKS[0])
                 if 2 <= x < HALF_STEPS + 2:
                     round_conv(x - 2)
                 if products:
+                    scalar_products(x, SCALAR_CHUNKS[0])
                     vector_products(x, VECTOR_CHUNKS[0])
                 if first and taps_ahead:
                     group_inputs(j + 1)
@@ -370,11 +369,9 @@ def tile_multiheadattention820_pa_t_kernel(tc, v, attn_out, dyn_w, dyn_b, out_pr
                     scalar_products(x, SCALAR_CHUNKS[1])
                 if additions:
                     add_up(x - 1, 2)
-                if first and taps_ahead:
-                    logits_of(j + 1)
-                if second and 1 <= j <= LC:
-                    project(j - 1)
-                if additions:
                     add_up(x - 1, 3)
                 if first and taps_ahead:
+                    logits_of(j + 1)
                     shift_logits(j + 1)
+                if second and 1 <= j <= LC:
+                    project(j - 1)

@@ -23,6 +23,7 @@ WIN = LC + K - 1
 CHUNKS = E // P
 HEADS_PER_CHUNK = P // R
 WORDS = E // 2
+HALF_STEPS = B * LC
 J_ATTN = 2
 V_ROWS = 8
 SCALAR_CHUNKS = (0, 3)
@@ -44,6 +45,12 @@ def tile_multiheadattention820_pa_t_kernel(tc, v, attn_out, dyn_w, dyn_b, out_pr
 
     with ExitStack() as ctx:
         keep = ctx.enter_context(tc.tile_pool(name="keep", bufs=1))
+        loads = ctx.enter_context(tc.tile_pool(name="loads", bufs=2))
+        work = ctx.enter_context(tc.tile_pool(name="work", bufs=2))
+        words_ps = ctx.enter_context(tc.psum_pool(name="words_ps", bufs=1))
+        logit_ps = ctx.enter_context(tc.psum_pool(name="logit_ps", bufs=1))
+        conv_ps = ctx.enter_context(tc.psum_pool(name="conv_ps", bufs=3))
+        out_ps = ctx.enter_context(tc.psum_pool(name="out_ps", bufs=1))
 
         v_sb = keep.tile([P, WIN, B, E], BF16)
         ident_f32 = keep.tile([P, P], F32)
@@ -62,82 +69,13 @@ def tile_multiheadattention820_pa_t_kernel(tc, v, attn_out, dyn_w, dyn_b, out_pr
         dyn_bias = keep.tile([P, H * K], F32)
         out_bias = keep.tile([P, E], F32)
 
-        loads = ctx.enter_context(tc.tile_pool(name="loads", bufs=2))
         attn_tiles = {}
+        step = {}
+        half = {}
 
         def load_attn(j):
             attn_tiles[j] = loads.tile([P, J_ATTN, B, E], BF16, tag="attn", name="attn_sb")
             nc.sync.dma_start(out=attn_tiles[j][:], in_=attn_rows[:, j : j + J_ATTN, :, :])
-
-        with tc.tile_pool(name="prep", bufs=1) as prep, tc.psum_pool(name="prep_ps", bufs=2) as prep_ps:
-            dw_raw = prep.tile([P, 2, E], BF16)
-            nc.sync.dma_start(out=dw_raw[:], in_=dyn_w.rearrange("(g p) e -> p g e", p=P))
-            nc.sync.dma_start(out=v_sb[:, PAD_L : PAD_L + V_ROWS, :, :], in_=v_rows[:, 0:V_ROWS, :, :])
-            load_attn(0)
-            db_raw = prep.tile([P, H * K], BF16)
-            nc.sync.dma_start(out=db_raw[:], in_=dyn_b.partition_broadcast(P))
-            nc.sync.dma_start(out=v_sb[1:113, 0:PAD_L, :, :], in_=v_rows[0:112, LC - PAD_L : LC, :, :])
-            nc.sync.dma_start(out=v_sb[113:P, 0:PAD_L, :, :], in_=v_rows[112 : P - 1, LC - PAD_L : LC, :, :])
-            ow_raw = prep.tile([P, CHUNKS, 2 * E], BF16)
-            nc.sync.dma_start(out=ow_raw[:], in_=out_proj_w.rearrange("(g p) k -> p g k", p=P))
-            ob_raw = prep.tile([P, E], BF16)
-            nc.sync.dma_start(out=ob_raw[:], in_=out_proj_b.partition_broadcast(P))
-            for l0 in range(V_ROWS, LC, V_ROWS):
-                nc.sync.dma_start(
-                    out=v_sb[:, PAD_L + l0 : PAD_L + l0 + V_ROWS, :, :], in_=v_rows[:, l0 : l0 + V_ROWS, :, :]
-                )
-            nc.sync.dma_start(out=v_sb[0:112, PAD_L + LC : WIN, :, :], in_=v_rows[1:113, 0:PAD_R, :, :])
-            nc.sync.dma_start(out=v_sb[112 : P - 1, PAD_L + LC : WIN, :, :], in_=v_rows[113:P, 0:PAD_R, :, :])
-
-            nc.vector.tensor_copy(out=dyn_bias[:], in_=db_raw[:])
-            nc.vector.tensor_copy(out=out_bias[:], in_=ob_raw[:])
-
-            dw_grp = prep.tile([P, H * K, PACK], BF16, align_bytes=64)
-            dw_words = dw_raw[:].bitcast(F32)
-            dw_bank = prep_ps.tile([P, 2, 2 * P], F32, tag="words")
-            for g in range(2):
-                transpose_words(nc, dw_bank[:, :, g * P : (g + 1) * P], dw_words[:, g, :], ident_f32)
-            nc.vector.tensor_copy(out=dw_grp[:].bitcast(F32), in_=dw_bank[:].rearrange("q u n -> q n u"))
-            nc.vector.quantize_mx(
-                out=dw_codes[:].bitcast(FP8X4), scales=dw_scales[:], in_=dw_grp[:].rearrange("q n t -> q (n t)")
-            )
-
-            w1_grp = prep.tile([P, E, PACK], BF16, align_bytes=64)
-            w2_grp = prep.tile([P, E, PACK], BF16, align_bytes=64)
-            ow_words = ow_raw[:].bitcast(F32)
-            for half in range(2):
-                cols = slice(half * 2 * P, (half + 1) * 2 * P)
-                w1_bank = prep_ps.tile([P, 2, 2 * P], F32, tag="words")
-                w2_bank = prep_ps.tile([P, PACK, 2 * P], BF16, tag="chunks")
-                for g in range(2):
-                    rows = 2 * half + g
-                    transpose_words(nc, w1_bank[:, :, g * P : (g + 1) * P], ow_words[:, rows, 0:WORDS], ident_f32)
-                    for c in range(CHUNKS):
-                        nc.tensor.transpose(
-                            w2_bank[:, c, g * P : (g + 1) * P],
-                            ow_raw[:, rows, E + c * P : E + (c + 1) * P],
-                            ident_bf16[:],
-                        )
-                nc.vector.tensor_copy(
-                    out=w1_grp[:, cols, :].bitcast(F32), in_=w1_bank[:].rearrange("q u n -> q n u")
-                )
-                nc.vector.tensor_copy(out=w2_grp[:, cols, :], in_=w2_bank[:].rearrange("q c n -> q n c"))
-            nc.vector.quantize_mx(
-                out=w1_codes[:].bitcast(FP8X4), scales=w1_scales[:], in_=w1_grp[:].rearrange("q n t -> q (n t)")
-            )
-            nc.vector.quantize_mx(
-                out=w2_codes[:].bitcast(FP8X4), scales=w2_scales[:], in_=w2_grp[:].rearrange("q n t -> q (n t)")
-            )
-
-        work = ctx.enter_context(tc.tile_pool(name="work", bufs=2))
-        prods = ctx.enter_context(tc.tile_pool(name="prods", bufs=2))
-        words_ps = ctx.enter_context(tc.psum_pool(name="words_ps", bufs=1))
-        logit_ps = ctx.enter_context(tc.psum_pool(name="logit_ps", bufs=1))
-        conv_ps = ctx.enter_context(tc.psum_pool(name="conv_ps", bufs=3))
-        out_ps = ctx.enter_context(tc.psum_pool(name="out_ps", bufs=1))
-
-        step = {}
-        half = {}
 
         def flip_inputs(j):
             attn_sb = attn_tiles[j - j % J_ATTN]
@@ -320,58 +258,132 @@ def tile_multiheadattention820_pa_t_kernel(tc, v, attn_out, dyn_w, dyn_b, out_pr
                 nc.vector.tensor_tensor(out=out_sb[:, b, :], in0=step[j]["acc%d" % b][:], in1=out_bias[:], op=ALU.add)
             nc.sync.dma_start(out=out_rows[:, j, :, :], in_=out_sb[:])
 
-        HALF_STEPS = B * LC
-        flip_inputs(0)
-        group_inputs(0)
-        quantise_inputs(0)
-        logits_of(0)
-        shift_logits(0)
-        exponentials(0)
-        normalise(0)
+        with tc.tile_pool(name="prep", bufs=1) as prep:
+            dw_raw = prep.tile([P, 2, E], BF16)
+            nc.sync.dma_start(out=dw_raw[:], in_=dyn_w.rearrange("(g p) e -> p g e", p=P))
+            nc.sync.dma_start(out=v_sb[:, PAD_L : PAD_L + V_ROWS, :, :], in_=v_rows[:, 0:V_ROWS, :, :])
+            load_attn(0)
+            db_raw = prep.tile([P, H * K], BF16)
+            nc.sync.dma_start(out=db_raw[:], in_=dyn_b.partition_broadcast(P))
+            nc.sync.dma_start(out=v_sb[1:113, 0:PAD_L, :, :], in_=v_rows[0:112, LC - PAD_L : LC, :, :])
+            nc.sync.dma_start(out=v_sb[113:P, 0:PAD_L, :, :], in_=v_rows[112 : P - 1, LC - PAD_L : LC, :, :])
+            nc.sync.dma_start(
+                out=v_sb[:, PAD_L + V_ROWS : PAD_L + 2 * V_ROWS, :, :], in_=v_rows[:, V_ROWS : 2 * V_ROWS, :, :]
+            )
+            load_attn(J_ATTN)
+            ow_raw = prep.tile([P, CHUNKS, 2 * E], BF16)
+            nc.sync.dma_start(out=ow_raw[:], in_=out_proj_w.rearrange("(g p) k -> p g k", p=P))
+            ob_raw = prep.tile([P, E], BF16)
+            nc.sync.dma_start(out=ob_raw[:], in_=out_proj_b.partition_broadcast(P))
+            for l0 in range(2 * V_ROWS, LC, V_ROWS):
+                nc.sync.dma_start(
+                    out=v_sb[:, PAD_L + l0 : PAD_L + l0 + V_ROWS, :, :], in_=v_rows[:, l0 : l0 + V_ROWS, :, :]
+                )
+            nc.sync.dma_start(out=v_sb[0:112, PAD_L + LC : WIN, :, :], in_=v_rows[1:113, 0:PAD_R, :, :])
+            nc.sync.dma_start(out=v_sb[112 : P - 1, PAD_L + LC : WIN, :, :], in_=v_rows[113:P, 0:PAD_R, :, :])
+
+            nc.vector.tensor_copy(out=dyn_bias[:], in_=db_raw[:])
+            dw_grp = prep.tile([P, H * K, PACK], BF16, align_bytes=64)
+            dw_words = dw_raw[:].bitcast(F32)
+            dw_bank = words_ps.tile([P, 2, 2 * P], F32, tag="v_bank")
+            for g in range(2):
+                transpose_words(nc, dw_bank[:, :, g * P : (g + 1) * P], dw_words[:, g, :], ident_f32)
+            nc.vector.tensor_copy(out=dw_grp[:].bitcast(F32), in_=dw_bank[:].rearrange("q u n -> q n u"))
+            nc.vector.quantize_mx(
+                out=dw_codes[:].bitcast(FP8X4), scales=dw_scales[:], in_=dw_grp[:].rearrange("q n t -> q (n t)")
+            )
+
+            flip_inputs(0)
+            group_inputs(0)
+            quantise_inputs(0)
+            logits_of(0)
+            shift_logits(0)
+            exponentials(0)
+            normalise(0)
+            flip_inputs(1)
+            group_inputs(1)
+            quantise_inputs(1)
+            logits_of(1)
+
+            nc.vector.tensor_copy(out=out_bias[:], in_=ob_raw[:])
+            w1_grp = prep.tile([P, E, PACK], BF16, align_bytes=64)
+            w2_grp = prep.tile([P, E, PACK], BF16, align_bytes=64)
+            ow_words = ow_raw[:].bitcast(F32)
+            for pair in range(2):
+                cols = slice(pair * 2 * P, (pair + 1) * 2 * P)
+                w1_bank = words_ps.tile([P, 2, 2 * P], F32, tag="v_bank")
+                w2_bank = words_ps.tile([P, PACK, 2 * P], BF16, tag="a_bank")
+                for g in range(2):
+                    rows = 2 * pair + g
+                    transpose_words(nc, w1_bank[:, :, g * P : (g + 1) * P], ow_words[:, rows, 0:WORDS], ident_f32)
+                    for c in range(CHUNKS):
+                        nc.tensor.transpose(
+                            w2_bank[:, c, g * P : (g + 1) * P],
+                            ow_raw[:, rows, E + c * P : E + (c + 1) * P],
+                            ident_bf16[:],
+                        )
+                nc.vector.tensor_copy(
+                    out=w1_grp[:, cols, :].bitcast(F32), in_=w1_bank[:].rearrange("q u n -> q n u")
+                )
+                nc.vector.tensor_copy(out=w2_grp[:, cols, :], in_=w2_bank[:].rearrange("q c n -> q n c"))
+            nc.vector.quantize_mx(
+                out=w1_codes[:].bitcast(FP8X4), scales=w1_scales[:], in_=w1_grp[:].rearrange("q n t -> q (n t)")
+            )
+            nc.vector.quantize_mx(
+                out=w2_codes[:].bitcast(FP8X4), scales=w2_scales[:], in_=w2_grp[:].rearrange("q n t -> q (n t)")
+            )
+
+        prods = ctx.enter_context(tc.tile_pool(name="prods", bufs=2, reuse_waits="tile"))
+
         with tc.manual_schedule():
             for x in range(HALF_STEPS + 3):
                 j, b = divmod(x, B)
                 first, second = b == 0, b == 1
                 products = x < HALF_STEPS
                 additions = 1 <= x <= HALF_STEPS
-                taps_ahead = j + 1 < LC
+                rounding = 2 <= x < HALF_STEPS + 2
+                softmax_next = first and j + 1 < LC
+                inputs_after = second and j + 2 < LC
+                projecting = second and 1 <= j <= LC
+                storing = first and 2 <= j <= LC + 1
                 if products:
                     half[x] = {}
-                if first and j + J_ATTN < LC and j % J_ATTN == 0:
-                    load_attn(j + J_ATTN)
-                if first and taps_ahead:
-                    flip_inputs(j + 1)
-                if second and taps_ahead:
-                    exponentials(j + 1)
-                if 2 <= x < HALF_STEPS + 2:
+                if first and j % J_ATTN == 1 and j + 3 < LC:
+                    load_attn(j + 3)
+                if inputs_after:
+                    flip_inputs(j + 2)
+                if rounding:
                     round_conv(x - 2)
                 if products:
                     scalar_products(x, SCALAR_CHUNKS[0])
                     vector_products(x, VECTOR_CHUNKS[0])
-                if first and taps_ahead:
-                    group_inputs(j + 1)
+                if softmax_next:
+                    shift_logits(j + 1)
+                    exponentials(j + 1)
+                if inputs_after:
+                    group_inputs(j + 2)
                 if additions:
                     add_up(x - 1, 0)
                     add_up(x - 1, 1)
-                if second and taps_ahead:
-                    normalise(j + 1)
-                if second and 1 <= j <= LC:
+                if projecting:
                     quantise_conv(j - 1)
                 if products:
                     vector_products(x, VECTOR_CHUNKS[1])
-                if first and taps_ahead:
-                    quantise_inputs(j + 1)
-                if first and 2 <= j <= LC + 1:
+                if inputs_after:
+                    quantise_inputs(j + 2)
+                if storing:
                     store(j - 2)
                 if products:
                     vector_fold(x, VECTOR_CHUNKS[0])
+                if softmax_next:
+                    normalise(j + 1)
+                if products:
                     vector_fold(x, VECTOR_CHUNKS[1])
                     scalar_products(x, SCALAR_CHUNKS[1])
                 if additions:
                     add_up(x - 1, 2)
                     add_up(x - 1, 3)
-                if first and taps_ahead:
-                    logits_of(j + 1)
-                    shift_logits(j + 1)
-                if second and 1 <= j <= LC:
+                if projecting:
                     project(j - 1)
+                if inputs_after:
+                    logits_of(j + 2)

@@ -26,8 +26,8 @@ WORDS = E // 2
 HALF_STEPS = B * LC
 J_ATTN = 2
 V_ROWS = 8
-SCALAR_CHUNKS = (0, 3)
-VECTOR_CHUNKS = (1, 2)
+SCALAR_CHUNK, VECTOR_CHUNKS, SHARED_CHUNK = 0, (1, 2), 3
+SHARED_BY_VECTOR = 1
 
 FLOPS = 2 * T * B * (E * H * K + 2 * E * E + E * K)
 
@@ -160,14 +160,12 @@ def tile_multiheadattention820_pa_t_kernel(tc, v, attn_out, dyn_w, dyn_b, out_pr
             )
 
         def new_products(x, c):
-            prod = prods.tile([P, K, P], F32, tag="prod%d" % c, name="prod%d" % c)
-            half[x][c] = prod
-            return prod
+            half[x][c] = prods.tile([P, K, P], F32, tag="prod%d" % c, name="prod%d" % c)
 
-        def scalar_products(x, c):
+        def scalar_products(x, c, first_head):
             j, b = divmod(x, B)
-            prod = new_products(x, c)
-            for h in range(HEADS_PER_CHUNK):
+            prod = half[x][c]
+            for h in range(first_head, HEADS_PER_CHUNK):
                 head = c * HEADS_PER_CHUNK + h
                 for k in range(K):
                     nc.scalar.activation(
@@ -177,38 +175,31 @@ def tile_multiheadattention820_pa_t_kernel(tc, v, attn_out, dyn_w, dyn_b, out_pr
                         scale=step[j]["taps"][:, b, head, k : k + 1],
                     )
 
-        def vector_products(x, c):
+        def vector_products(x, c, count):
             j, b = divmod(x, B)
-            prod = new_products(x, c)
-            heads = slice(c * HEADS_PER_CHUNK, (c + 1) * HEADS_PER_CHUNK)
+            prod = half[x][c]
+            heads = slice(c * HEADS_PER_CHUNK, c * HEADS_PER_CHUNK + count)
             nc.vector.tensor_tensor(
-                out=prod[:].rearrange("p k (h r) -> p k h r", r=R),
-                in0=v_sb[:, j : j + K, b, c * P : (c + 1) * P].rearrange("p k (h r) -> p k h r", r=R),
+                out=prod[:, :, 0 : count * R].rearrange("p k (h r) -> p k h r", r=R),
+                in0=v_sb[:, j : j + K, b, c * P : c * P + count * R].rearrange("p k (h r) -> p k h r", r=R),
                 in1=step[j]["taps"][:, b, heads, :]
                 .rearrange("p h k -> p k h")
                 .unsqueeze(3)
-                .to_broadcast([P, K, HEADS_PER_CHUNK, R]),
+                .to_broadcast([P, K, count, R]),
                 op=ALU.mult,
-            )
-
-        def vector_fold(x, c):
-            prod = half[x][c]
-            nc.vector.tensor_tensor(
-                out=prod[:, 0 : K // 2, :], in0=prod[:, 0 : K // 2, :], in1=prod[:, K // 2 : K, :], op=ALU.add
             )
 
         def add_up(x, c):
             if c == 0:
                 half[x]["conv_t"] = conv_ps.tile([P, CHUNKS, P], F32, tag="conv_t", name="conv_t")
-            left = K // 2 if c in VECTOR_CHUNKS else K
-            for k in range(left):
+            for k in range(K):
                 nc.tensor.matmul(
                     out=half[x]["conv_t"][:, c, :],
                     lhsT=half[x][c][:, k, :],
                     rhs=ident_f32[:],
                     is_transpose=True,
                     start=(k == 0),
-                    stop=(k == left - 1),
+                    stop=(k == K - 1),
                 )
 
         def round_conv(x):
@@ -355,8 +346,10 @@ def tile_multiheadattention820_pa_t_kernel(tc, v, attn_out, dyn_w, dyn_b, out_pr
                 if rounding:
                     round_conv(x - 2)
                 if products:
-                    scalar_products(x, SCALAR_CHUNKS[0])
-                    vector_products(x, VECTOR_CHUNKS[0])
+                    for c in range(CHUNKS):
+                        new_products(x, c)
+                    scalar_products(x, SCALAR_CHUNK, 0)
+                    vector_products(x, VECTOR_CHUNKS[0], HEADS_PER_CHUNK)
                 if softmax_next:
                     shift_logits(j + 1)
                     exponentials(j + 1)
@@ -368,18 +361,16 @@ def tile_multiheadattention820_pa_t_kernel(tc, v, attn_out, dyn_w, dyn_b, out_pr
                 if projecting:
                     quantise_conv(j - 1)
                 if products:
-                    vector_products(x, VECTOR_CHUNKS[1])
+                    vector_products(x, VECTOR_CHUNKS[1], HEADS_PER_CHUNK)
                 if inputs_after:
                     quantise_inputs(j + 2)
                 if storing:
                     store(j - 2)
-                if products:
-                    vector_fold(x, VECTOR_CHUNKS[0])
                 if softmax_next:
                     normalise(j + 1)
                 if products:
-                    vector_fold(x, VECTOR_CHUNKS[1])
-                    scalar_products(x, SCALAR_CHUNKS[1])
+                    vector_products(x, SHARED_CHUNK, SHARED_BY_VECTOR)
+                    scalar_products(x, SHARED_CHUNK, SHARED_BY_VECTOR)
                 if additions:
                     add_up(x - 1, 2)
                     add_up(x - 1, 3)

@@ -26,8 +26,7 @@ WORDS = E // 2
 HALF_STEPS = B * LC
 J_ATTN = 2
 V_ROWS = 8
-SCALAR_CHUNK, VECTOR_CHUNKS, SHARED_CHUNK = 0, (1, 2), 3
-SHARED_BY_VECTOR = 1
+SCALAR_CHUNK, VECTOR_CHUNKS, GPSIMD_CHUNK = 0, (1, 2), 3
 
 FLOPS = 2 * T * B * (E * H * K + 2 * E * E + E * K)
 
@@ -47,9 +46,10 @@ def tile_multiheadattention820_pa_t_kernel(tc, v, attn_out, dyn_w, dyn_b, out_pr
         keep = ctx.enter_context(tc.tile_pool(name="keep", bufs=1))
         loads = ctx.enter_context(tc.tile_pool(name="loads", bufs=2))
         work = ctx.enter_context(tc.tile_pool(name="work", bufs=2))
-        words_ps = ctx.enter_context(tc.psum_pool(name="words_ps", bufs=1))
+        flip_ps = ctx.enter_context(tc.psum_pool(name="flip_ps", bufs=1))
         logit_ps = ctx.enter_context(tc.psum_pool(name="logit_ps", bufs=1))
-        conv_ps = ctx.enter_context(tc.psum_pool(name="conv_ps", bufs=3))
+        taps_ps = ctx.enter_context(tc.psum_pool(name="taps_ps", bufs=2))
+        conv_ps = ctx.enter_context(tc.psum_pool(name="conv_ps", bufs=2))
         out_ps = ctx.enter_context(tc.psum_pool(name="out_ps", bufs=1))
 
         v_sb = keep.tile([P, WIN, B, E], BF16)
@@ -77,40 +77,35 @@ def tile_multiheadattention820_pa_t_kernel(tc, v, attn_out, dyn_w, dyn_b, out_pr
             attn_tiles[j] = loads.tile([P, J_ATTN, B, E], BF16, tag="attn", name="attn_sb")
             nc.sync.dma_start(out=attn_tiles[j][:], in_=attn_rows[:, j : j + J_ATTN, :, :])
 
-        def flip_inputs(j):
-            attn_sb = attn_tiles[j - j % J_ATTN]
-            rows = {"v": v_sb[:, PAD_L + j, :, :].bitcast(F32), "a": attn_sb[:, j % J_ATTN, :, :].bitcast(F32)}
-            step[j] = {}
-            for name in ("v", "a"):
-                bank = words_ps.tile([P, B, 2, P], F32, tag=name + "_bank", name=name + "_bank")
-                for b in range(B):
-                    transpose_words(nc, bank[:, b, :, :], rows[name][:, b, :], ident_f32)
-                step[j][name + "_bank"] = bank
+        def flip_input(j, name):
+            step.setdefault(j, {})
+            if name == "v":
+                rows = v_sb[:, PAD_L + j, :, :].bitcast(F32)
+            else:
+                rows = attn_tiles[j - j % J_ATTN][:, j % J_ATTN, :, :].bitcast(F32)
+            bank = flip_ps.tile([P, B, 2, P], F32, tag="flip", name="flip_bank")
+            for b in range(B):
+                transpose_words(nc, bank[:, b, :, :], rows[:, b, :], ident_f32)
+            step[j][name + "_bank"] = bank
 
-        def group_inputs(j):
-            for name in ("v", "a"):
-                grouped = work.tile([P, B, P, PACK], BF16, align_bytes=64, tag=name + "_grp", name=name + "_grp")
-                nc.scalar.copy(
-                    out=grouped[:].bitcast(F32), in_=step[j][name + "_bank"][:].rearrange("q b u n -> q b n u")
-                )
-                step[j][name + "_grp"] = grouped
+        def group_input(j, name):
+            grouped = work.tile([P, B, P, PACK], BF16, align_bytes=64, tag=name + "_grp", name=name + "_grp")
+            nc.scalar.copy(
+                out=grouped[:].bitcast(F32), in_=step[j][name + "_bank"][:].rearrange("q b u n -> q b n u")
+            )
+            step[j][name + "_grp"] = grouped
 
-        def quantise_inputs(j):
-            for name in ("v", "a"):
-                slots = 2 if name == "v" else 4
-                codes = work.tile(
-                    [P, B * P], U32, align_bytes=64, tag=name + "_codes", name=name + "_codes", bufs=slots
-                )
-                scales = work.tile(
-                    [P, B * P], U8, align_bytes=64, tag=name + "_scales", name=name + "_scales", bufs=slots
-                )
-                nc.vector.quantize_mx(
-                    out=codes[:].bitcast(FP8X4),
-                    scales=scales[:],
-                    in_=step[j][name + "_grp"][:].rearrange("q b n t -> q (b n t)"),
-                )
-                step[j][name + "_codes"] = codes
-                step[j][name + "_scales"] = scales
+        def quantise_input(j, name):
+            slots = 2 if name == "v" else 5
+            codes = work.tile([P, B * P], U32, align_bytes=64, tag=name + "_codes", name=name + "_codes", bufs=slots)
+            scales = work.tile([P, B * P], U8, align_bytes=64, tag=name + "_scales", name=name + "_scales", bufs=slots)
+            nc.vector.quantize_mx(
+                out=codes[:].bitcast(FP8X4),
+                scales=scales[:],
+                in_=step[j][name + "_grp"][:].rearrange("q b n t -> q (b n t)"),
+            )
+            step[j][name + "_codes"] = codes
+            step[j][name + "_scales"] = scales
 
         def logits_of(j):
             logits = logit_ps.tile([P, B, H * K], F32, tag="logits")
@@ -130,7 +125,7 @@ def tile_multiheadattention820_pa_t_kernel(tc, v, attn_out, dyn_w, dyn_b, out_pr
         def by_head(taps):
             return taps[:].rearrange("p b h k -> p (b h) k")
 
-        def shift_logits(j):
+        def bias_and_top(j):
             taps = work.tile([P, B, H, K], F32, tag="taps")
             nc.vector.tensor_tensor(
                 out=taps[:].rearrange("p b h k -> p b (h k)"),
@@ -140,32 +135,55 @@ def tile_multiheadattention820_pa_t_kernel(tc, v, attn_out, dyn_w, dyn_b, out_pr
             )
             top = work.tile([P, B * H], F32, tag="top")
             nc.vector.tensor_reduce(out=top[:], in_=by_head(taps), axis=AXIS_X, op=ALU.max)
-            nc.vector.tensor_tensor(
-                out=by_head(taps), in0=by_head(taps), in1=top[:].unsqueeze(2).to_broadcast([P, B * H, K]), op=ALU.subtract
-            )
             step[j]["taps"] = taps
+            step[j]["top"] = top
+
+        def each_head(j, op, per_head):
+            taps = step[j]["taps"]
+            nc.gpsimd.tensor_tensor(
+                out=by_head(taps),
+                in0=by_head(taps),
+                in1=step[j][per_head][:].unsqueeze(2).to_broadcast([P, B * H, K]),
+                op=op,
+            )
 
         def exponentials(j):
             flat = step[j]["taps"][:].rearrange("p b h k -> p (b h k)")
             nc.scalar.activation(out=flat, in_=flat, func=ACT.Exp)
 
-        def normalise(j):
-            taps = step[j]["taps"]
+        def inverse_sums(j):
             total = work.tile([P, B * H], F32, tag="total")
-            nc.vector.tensor_reduce(out=total[:], in_=by_head(taps), axis=AXIS_X, op=ALU.add)
+            nc.vector.tensor_reduce(out=total[:], in_=by_head(step[j]["taps"]), axis=AXIS_X, op=ALU.add)
             inverse = work.tile([P, B * H], F32, tag="inverse")
             nc.vector.reciprocal(out=inverse[:], in_=total[:])
-            nc.vector.tensor_tensor(
-                out=by_head(taps), in0=by_head(taps), in1=inverse[:].unsqueeze(2).to_broadcast([P, B * H, K]), op=ALU.mult
-            )
+            step[j]["inverse"] = inverse
+
+        def flip_taps(j):
+            flat = step[j]["taps"][:].rearrange("p b h k -> p (b h k)")
+            bank = flip_ps.tile([P, PACK, P], F32, tag="flip", name="flip_bank")
+            for q in range(PACK):
+                nc.tensor.transpose(bank[:, q, :], flat[:, q * P : (q + 1) * P], ident_f32[:])
+            step[j]["taps_bank"] = bank
+
+        def copy_flipped_taps(j):
+            flipped = work.tile([P, PACK, P], F32, tag="flipped", bufs=1)
+            nc.scalar.copy(out=flipped[:], in_=step[j]["taps_bank"][:])
+            step[j]["flipped"] = flipped
+
+        def flip_taps_back(j):
+            taps = taps_ps.tile([P, B, H, K], F32, tag="taps_ps", name="taps_bank")
+            flat = taps[:].rearrange("p b h k -> p (b h k)")
+            for q in range(PACK):
+                nc.tensor.transpose(flat[:, q * P : (q + 1) * P], step[j]["flipped"][:, q, :], ident_f32[:])
+            step[j]["taps_ps"] = taps
 
         def new_products(x, c):
             half[x][c] = prods.tile([P, K, P], F32, tag="prod%d" % c, name="prod%d" % c)
 
-        def scalar_products(x, c, first_head):
+        def scalar_products(x, c, heads):
             j, b = divmod(x, B)
             prod = half[x][c]
-            for h in range(first_head, HEADS_PER_CHUNK):
+            for h in heads:
                 head = c * HEADS_PER_CHUNK + h
                 for k in range(K):
                     nc.scalar.activation(
@@ -175,19 +193,25 @@ def tile_multiheadattention820_pa_t_kernel(tc, v, attn_out, dyn_w, dyn_b, out_pr
                         scale=step[j]["taps"][:, b, head, k : k + 1],
                     )
 
-        def vector_products(x, c, count):
+        def wide_products(engine, taps, x, c, first, count):
             j, b = divmod(x, B)
-            prod = half[x][c]
-            heads = slice(c * HEADS_PER_CHUNK, c * HEADS_PER_CHUNK + count)
-            nc.vector.tensor_tensor(
-                out=prod[:, :, 0 : count * R].rearrange("p k (h r) -> p k h r", r=R),
-                in0=v_sb[:, j : j + K, b, c * P : c * P + count * R].rearrange("p k (h r) -> p k h r", r=R),
-                in1=step[j]["taps"][:, b, heads, :]
+            channels = slice(first * R, (first + count) * R)
+            head = c * HEADS_PER_CHUNK + first
+            engine.tensor_tensor(
+                out=half[x][c][:, :, channels].rearrange("p k (h r) -> p k h r", r=R),
+                in0=v_sb[:, j : j + K, b, head * R : (head + count) * R].rearrange("p k (h r) -> p k h r", r=R),
+                in1=step[j][taps][:, b, head : head + count, :]
                 .rearrange("p h k -> p k h")
                 .unsqueeze(3)
                 .to_broadcast([P, K, count, R]),
                 op=ALU.mult,
             )
+
+        def vector_products(x, c):
+            wide_products(nc.vector, "taps_ps", x, c, 0, HEADS_PER_CHUNK)
+
+        def gpsimd_products(x, h):
+            wide_products(nc.gpsimd, "taps", x, GPSIMD_CHUNK, h, 1)
 
         def add_up(x, c):
             if c == 0:
@@ -276,7 +300,7 @@ def tile_multiheadattention820_pa_t_kernel(tc, v, attn_out, dyn_w, dyn_b, out_pr
             nc.vector.tensor_copy(out=dyn_bias[:], in_=db_raw[:])
             dw_grp = prep.tile([P, H * K, PACK], BF16, align_bytes=64)
             dw_words = dw_raw[:].bitcast(F32)
-            dw_bank = words_ps.tile([P, 2, 2 * P], F32, tag="v_bank")
+            dw_bank = flip_ps.tile([P, 2, 2 * P], F32, tag="flip", name="flip_bank")
             for g in range(2):
                 transpose_words(nc, dw_bank[:, :, g * P : (g + 1) * P], dw_words[:, g, :], ident_f32)
             nc.vector.tensor_copy(out=dw_grp[:].bitcast(F32), in_=dw_bank[:].rearrange("q u n -> q n u"))
@@ -284,17 +308,23 @@ def tile_multiheadattention820_pa_t_kernel(tc, v, attn_out, dyn_w, dyn_b, out_pr
                 out=dw_codes[:].bitcast(FP8X4), scales=dw_scales[:], in_=dw_grp[:].rearrange("q n t -> q (n t)")
             )
 
-            flip_inputs(0)
-            group_inputs(0)
-            quantise_inputs(0)
-            logits_of(0)
-            shift_logits(0)
-            exponentials(0)
-            normalise(0)
-            flip_inputs(1)
-            group_inputs(1)
-            quantise_inputs(1)
-            logits_of(1)
+            for j in range(2):
+                for name in ("v", "a"):
+                    flip_input(j, name)
+                    group_input(j, name)
+                    quantise_input(j, name)
+                logits_of(j)
+                if j == 0:
+                    bias_and_top(0)
+                    each_head(0, ALU.subtract, "top")
+                    exponentials(0)
+                    inverse_sums(0)
+                    each_head(0, ALU.mult, "inverse")
+            flip_input(2, "v")
+            group_input(2, "v")
+            flip_taps(0)
+            copy_flipped_taps(0)
+            flip_taps_back(0)
 
             nc.vector.tensor_copy(out=out_bias[:], in_=ob_raw[:])
             w1_grp = prep.tile([P, E, PACK], BF16, align_bytes=64)
@@ -302,8 +332,8 @@ def tile_multiheadattention820_pa_t_kernel(tc, v, attn_out, dyn_w, dyn_b, out_pr
             ow_words = ow_raw[:].bitcast(F32)
             for pair in range(2):
                 cols = slice(pair * 2 * P, (pair + 1) * 2 * P)
-                w1_bank = words_ps.tile([P, 2, 2 * P], F32, tag="v_bank")
-                w2_bank = words_ps.tile([P, PACK, 2 * P], BF16, tag="a_bank")
+                w1_bank = out_ps.tile([P, 2, 2 * P], F32, tag="acc0")
+                w2_bank = out_ps.tile([P, PACK, 2 * P], BF16, tag="acc1")
                 for g in range(2):
                     rows = 2 * pair + g
                     transpose_words(nc, w1_bank[:, :, g * P : (g + 1) * P], ow_words[:, rows, 0:WORDS], ident_f32)
@@ -327,54 +357,84 @@ def tile_multiheadattention820_pa_t_kernel(tc, v, attn_out, dyn_w, dyn_b, out_pr
         prods = ctx.enter_context(tc.tile_pool(name="prods", bufs=2, reuse_waits="tile"))
 
         with tc.manual_schedule():
-            for x in range(HALF_STEPS + 3):
+            for x in range(HALF_STEPS + 4):
                 j, b = divmod(x, B)
-                first, second = b == 0, b == 1
                 products = x < HALF_STEPS
                 additions = 1 <= x <= HALF_STEPS
                 rounding = 2 <= x < HALF_STEPS + 2
-                softmax_next = first and j + 1 < LC
-                inputs_after = second and j + 2 < LC
-                projecting = second and 1 <= j <= LC
-                storing = first and 2 <= j <= LC + 1
+                softmax_next = j + 1 < LC
+                inputs_after = j + 2 < LC
                 if products:
                     half[x] = {}
-                if first and j % J_ATTN == 1 and j + 3 < LC:
-                    load_attn(j + 3)
-                if inputs_after:
-                    flip_inputs(j + 2)
-                if rounding:
-                    round_conv(x - 2)
-                if products:
                     for c in range(CHUNKS):
                         new_products(x, c)
-                    scalar_products(x, SCALAR_CHUNK, 0)
-                    vector_products(x, VECTOR_CHUNKS[0], HEADS_PER_CHUNK)
-                if softmax_next:
-                    shift_logits(j + 1)
-                    exponentials(j + 1)
-                if inputs_after:
-                    group_inputs(j + 2)
-                if additions:
-                    add_up(x - 1, 0)
-                    add_up(x - 1, 1)
-                if projecting:
-                    quantise_conv(j - 1)
-                if products:
-                    vector_products(x, VECTOR_CHUNKS[1], HEADS_PER_CHUNK)
-                if inputs_after:
-                    quantise_inputs(j + 2)
-                if storing:
-                    store(j - 2)
-                if softmax_next:
-                    normalise(j + 1)
-                if products:
-                    vector_products(x, SHARED_CHUNK, SHARED_BY_VECTOR)
-                    scalar_products(x, SHARED_CHUNK, SHARED_BY_VECTOR)
-                if additions:
-                    add_up(x - 1, 2)
-                    add_up(x - 1, 3)
-                if projecting:
-                    project(j - 1)
-                if inputs_after:
-                    logits_of(j + 2)
+                if b == 0:
+                    if j % J_ATTN == 0 and j + 4 < LC:
+                        load_attn(j + 4)
+                    if inputs_after:
+                        flip_input(j + 2, "a")
+                    if softmax_next:
+                        bias_and_top(j + 1)
+                    if products:
+                        vector_products(x, VECTOR_CHUNKS[0])
+                        gpsimd_products(x, 0)
+                        scalar_products(x, SCALAR_CHUNK, (0,))
+                    if softmax_next:
+                        each_head(j + 1, ALU.subtract, "top")
+                    if rounding:
+                        round_conv(x - 2)
+                    if inputs_after:
+                        group_input(j + 2, "a")
+                    if softmax_next:
+                        exponentials(j + 1)
+                        inverse_sums(j + 1)
+                    if products:
+                        gpsimd_products(x, 1)
+                    if softmax_next:
+                        each_head(j + 1, ALU.mult, "inverse")
+                    if inputs_after:
+                        quantise_input(j + 2, "v")
+                        quantise_input(j + 2, "a")
+                    if additions:
+                        for c in range(CHUNKS):
+                            add_up(x - 1, c)
+                    if products:
+                        vector_products(x, VECTOR_CHUNKS[1])
+                        gpsimd_products(x, 2)
+                        gpsimd_products(x, 3)
+                        scalar_products(x, SCALAR_CHUNK, (1, 2, 3))
+                    if 0 <= j - 2 < LC:
+                        project(j - 2)
+                    if inputs_after:
+                        logits_of(j + 2)
+                else:
+                    if softmax_next:
+                        flip_taps(j + 1)
+                    if products:
+                        vector_products(x, VECTOR_CHUNKS[0])
+                        scalar_products(x, SCALAR_CHUNK, (0,))
+                    if additions:
+                        add_up(x - 1, 0)
+                    if softmax_next:
+                        copy_flipped_taps(j + 1)
+                        flip_taps_back(j + 1)
+                    if rounding:
+                        round_conv(x - 2)
+                    if 0 <= j - 2 < LC:
+                        store(j - 2)
+                    if products:
+                        vector_products(x, VECTOR_CHUNKS[1])
+                        scalar_products(x, SCALAR_CHUNK, (1, 2))
+                        for h in range(HEADS_PER_CHUNK):
+                            gpsimd_products(x, h)
+                    if j + 3 < LC:
+                        flip_input(j + 3, "v")
+                    if additions:
+                        for c in range(1, CHUNKS):
+                            add_up(x - 1, c)
+                    if j + 3 < LC:
+                        group_input(j + 3, "v")
+                    if products:
+                        scalar_products(x, SCALAR_CHUNK, (3,))
+                    if 0 <= j - 1 < LC:
+                        quantise_conv(j - 1)

@@ -26,7 +26,8 @@ WORDS = E // 2
 HALF_STEPS = B * LC
 J_ATTN = 2
 V_ROWS = 8
-SCALAR_CHUNK, VECTOR_CHUNKS, GPSIMD_CHUNK = 0, (1, 2), 3
+SCALAR_CHUNK, VECTOR_CHUNKS, SHARED_CHUNK = 0, (1, 2), 3
+GPSIMD_HEADS = 3
 
 FLOPS = 2 * T * B * (E * H * K + 2 * E * E + E * K)
 
@@ -211,7 +212,7 @@ def tile_multiheadattention820_pa_t_kernel(tc, v, attn_out, dyn_w, dyn_b, out_pr
             wide_products(nc.vector, "taps_ps", x, c, 0, HEADS_PER_CHUNK)
 
         def gpsimd_products(x, h):
-            wide_products(nc.gpsimd, "taps", x, GPSIMD_CHUNK, h, 1)
+            wide_products(nc.gpsimd, "taps", x, SHARED_CHUNK, h, 1)
 
         def add_up(x, c):
             if c == 0:
@@ -400,9 +401,10 @@ def tile_multiheadattention820_pa_t_kernel(tc, v, attn_out, dyn_w, dyn_b, out_pr
                             add_up(x - 1, c)
                     if products:
                         vector_products(x, VECTOR_CHUNKS[1])
-                        gpsimd_products(x, 2)
-                        gpsimd_products(x, 3)
+                        for h in range(2, GPSIMD_HEADS):
+                            gpsimd_products(x, h)
                         scalar_products(x, SCALAR_CHUNK, (1, 2, 3))
+                        scalar_products(x, SHARED_CHUNK, range(GPSIMD_HEADS, HEADS_PER_CHUNK))
                     if 0 <= j - 2 < LC:
                         project(j - 2)
                     if inputs_after:
@@ -425,7 +427,7 @@ def tile_multiheadattention820_pa_t_kernel(tc, v, attn_out, dyn_w, dyn_b, out_pr
                     if products:
                         vector_products(x, VECTOR_CHUNKS[1])
                         scalar_products(x, SCALAR_CHUNK, (1, 2))
-                        for h in range(HEADS_PER_CHUNK):
+                        for h in range(GPSIMD_HEADS):
                             gpsimd_products(x, h)
                     if j + 3 < LC:
                         flip_input(j + 3, "v")
@@ -436,5 +438,6 @@ def tile_multiheadattention820_pa_t_kernel(tc, v, attn_out, dyn_w, dyn_b, out_pr
                         group_input(j + 3, "v")
                     if products:
                         scalar_products(x, SCALAR_CHUNK, (3,))
+                        scalar_products(x, SHARED_CHUNK, range(GPSIMD_HEADS, HEADS_PER_CHUNK))
                     if 0 <= j - 1 < LC:
                         quantise_conv(j - 1)

@@ -230,7 +230,7 @@ def tile_multiheadattention820_pa_t_kernel(tc, v, attn_out, dyn_w, dyn_b, out_pr
         def round_conv(x):
             j, b = divmod(x, B)
             if b == 0:
-                step[j]["conv_grp"] = work.tile([P, B, P, PACK], BF16, align_bytes=64, tag="conv_grp", name="conv_grp")
+                step[j]["conv_grp"] = work.tile([P, B, P, PACK], BF16, align_bytes=64, tag="conv_grp", name="conv_grp", bufs=3)
             nc.scalar.copy(out=step[j]["conv_grp"][:, b, :, :], in_=half[x]["conv_t"][:].rearrange("q c n -> q n c"))
 
         def quantise_conv(j):
@@ -388,20 +388,20 @@ def tile_multiheadattention820_pa_t_kernel(tc, v, attn_out, dyn_w, dyn_b, out_pr
                         group_input(j + 2, "a")
                     if softmax_next:
                         exponentials(j + 1)
-                        inverse_sums(j + 1)
-                    if products:
-                        gpsimd_products(x, 1)
-                    if softmax_next:
-                        each_head(j + 1, ALU.mult, "inverse")
                     if inputs_after:
                         quantise_input(j + 2, "v")
                         quantise_input(j + 2, "a")
+                    if 0 <= j - 2 < LC:
+                        quantise_conv(j - 2)
+                    if softmax_next:
+                        inverse_sums(j + 1)
+                        each_head(j + 1, ALU.mult, "inverse")
                     if additions:
                         for c in range(CHUNKS):
                             add_up(x - 1, c)
                     if products:
                         vector_products(x, VECTOR_CHUNKS[1])
-                        for h in range(2, GPSIMD_HEADS):
+                        for h in range(1, GPSIMD_HEADS):
                             gpsimd_products(x, h)
                         scalar_products(x, SCALAR_CHUNK, (1, 2, 3))
                         scalar_products(x, SHARED_CHUNK, range(GPSIMD_HEADS, HEADS_PER_CHUNK))
@@ -439,5 +439,3 @@ def tile_multiheadattention820_pa_t_kernel(tc, v, attn_out, dyn_w, dyn_b, out_pr
                     if products:
                         scalar_products(x, SCALAR_CHUNK, (3,))
                         scalar_products(x, SHARED_CHUNK, range(GPSIMD_HEADS, HEADS_PER_CHUNK))
-                    if 0 <= j - 1 < LC:
-                        quantise_conv(j - 1)

@@ -26,8 +26,10 @@ WORDS = E // 2
 HALF_STEPS = B * LC
 J_ATTN = 2
 V_ROWS = 8
+V_FIRST = 2
 SCALAR_CHUNK, VECTOR_CHUNKS, SHARED_CHUNK = 0, (1, 2), 3
 GPSIMD_HEADS = 3
+VECTOR_HEADS = slice(4, 12)
 
 FLOPS = 2 * T * B * (E * H * K + 2 * E * E + E * K)
 
@@ -47,6 +49,8 @@ def tile_multiheadattention820_pa_t_kernel(tc, v, attn_out, dyn_w, dyn_b, out_pr
         keep = ctx.enter_context(tc.tile_pool(name="keep", bufs=1))
         loads = ctx.enter_context(tc.tile_pool(name="loads", bufs=2))
         work = ctx.enter_context(tc.tile_pool(name="work", bufs=2))
+        prep = ctx.enter_context(tc.tile_pool(name="prep", bufs=1))
+        prods = ctx.enter_context(tc.tile_pool(name="prods", bufs=2))
         flip_ps = ctx.enter_context(tc.psum_pool(name="flip_ps", bufs=1))
         logit_ps = ctx.enter_context(tc.psum_pool(name="logit_ps", bufs=1))
         taps_ps = ctx.enter_context(tc.psum_pool(name="taps_ps", bufs=2))
@@ -58,8 +62,7 @@ def tile_multiheadattention820_pa_t_kernel(tc, v, attn_out, dyn_w, dyn_b, out_pr
         make_identity(nc, ident_f32[:])
         ident_bf16 = keep.tile([P, P], BF16)
         make_identity(nc, ident_bf16[:])
-        nc.vector.memset(v_sb[0:1, 0:PAD_L, :, :], 0.0)
-        nc.gpsimd.memset(v_sb[96:P, PAD_L + LC : WIN, :, :], 0.0)
+        nc.gpsimd.memset(v_sb[0:1, 0:PAD_L, :, :].rearrange("p x b e -> p (x b e)").bitcast(F32), 0.0)
 
         dw_codes = keep.tile([P, H * K], U32, align_bytes=64)
         dw_scales = keep.tile([P, H * K], U8, align_bytes=64)
@@ -160,22 +163,23 @@ def tile_multiheadattention820_pa_t_kernel(tc, v, attn_out, dyn_w, dyn_b, out_pr
             step[j]["inverse"] = inverse
 
         def flip_taps(j):
-            flat = step[j]["taps"][:].rearrange("p b h k -> p (b h k)")
-            bank = flip_ps.tile([P, PACK, P], F32, tag="flip", name="flip_bank")
-            for q in range(PACK):
-                nc.tensor.transpose(bank[:, q, :], flat[:, q * P : (q + 1) * P], ident_f32[:])
+            bank = flip_ps.tile([P, B, P], F32, tag="flip", name="flip_bank")
+            for b in range(B):
+                rows = step[j]["taps"][:, b, VECTOR_HEADS, :].rearrange("p h k -> p (h k)")
+                nc.tensor.transpose(bank[:, b, :], rows, ident_f32[:])
             step[j]["taps_bank"] = bank
 
         def copy_flipped_taps(j):
-            flipped = work.tile([P, PACK, P], F32, tag="flipped", bufs=1)
+            flipped = work.tile([P, B, P], F32, tag="flipped", bufs=1)
             nc.scalar.copy(out=flipped[:], in_=step[j]["taps_bank"][:])
             step[j]["flipped"] = flipped
 
         def flip_taps_back(j):
-            taps = taps_ps.tile([P, B, H, K], F32, tag="taps_ps", name="taps_bank")
-            flat = taps[:].rearrange("p b h k -> p (b h k)")
-            for q in range(PACK):
-                nc.tensor.transpose(flat[:, q * P : (q + 1) * P], step[j]["flipped"][:, q, :], ident_f32[:])
+            taps = taps_ps.tile([P, B, P // K, K], F32, tag="taps_ps", name="taps_bank")
+            for b in range(B):
+                nc.tensor.transpose(
+                    taps[:, b, :, :].rearrange("p h k -> p (h k)"), step[j]["flipped"][:, b, :], ident_f32[:]
+                )
             step[j]["taps_ps"] = taps
 
         def new_products(x, c):
@@ -195,36 +199,46 @@ def tile_multiheadattention820_pa_t_kernel(tc, v, attn_out, dyn_w, dyn_b, out_pr
                     )
 
         def wide_products(engine, taps, x, c, first, count):
-            j, b = divmod(x, B)
+            j = x // B
             channels = slice(first * R, (first + count) * R)
             head = c * HEADS_PER_CHUNK + first
             engine.tensor_tensor(
                 out=half[x][c][:, :, channels].rearrange("p k (h r) -> p k h r", r=R),
-                in0=v_sb[:, j : j + K, b, head * R : (head + count) * R].rearrange("p k (h r) -> p k h r", r=R),
-                in1=step[j][taps][:, b, head : head + count, :]
-                .rearrange("p h k -> p k h")
-                .unsqueeze(3)
-                .to_broadcast([P, K, count, R]),
+                in0=v_sb[:, j : j + K, x % B, head * R : (head + count) * R].rearrange("p k (h r) -> p k h r", r=R),
+                in1=taps.rearrange("p h k -> p k h").unsqueeze(3).to_broadcast([P, K, count, R]),
                 op=ALU.mult,
             )
 
         def vector_products(x, c):
-            wide_products(nc.vector, "taps_ps", x, c, 0, HEADS_PER_CHUNK)
+            j, b = divmod(x, B)
+            first = c * HEADS_PER_CHUNK - VECTOR_HEADS.start
+            wide_products(
+                nc.vector, step[j]["taps_ps"][:, b, first : first + HEADS_PER_CHUNK, :], x, c, 0, HEADS_PER_CHUNK
+            )
 
         def gpsimd_products(x, h):
-            wide_products(nc.gpsimd, "taps", x, SHARED_CHUNK, h, 1)
+            j, b = divmod(x, B)
+            head = SHARED_CHUNK * HEADS_PER_CHUNK + h
+            wide_products(nc.gpsimd, step[j]["taps"][:, b, head : head + 1, :], x, SHARED_CHUNK, h, 1)
+
+        def gpsimd_fold(x):
+            prod = half[x][SHARED_CHUNK]
+            nc.gpsimd.tensor_tensor(
+                out=prod[:, 0 : K // 2, :], in0=prod[:, 0 : K // 2, :], in1=prod[:, K // 2 : K, :], op=ALU.add
+            )
 
         def add_up(x, c):
             if c == 0:
                 half[x]["conv_t"] = conv_ps.tile([P, CHUNKS, P], F32, tag="conv_t", name="conv_t")
-            for k in range(K):
+            left = K // 2 if c == SHARED_CHUNK and x % B == 0 else K
+            for k in range(left):
                 nc.tensor.matmul(
                     out=half[x]["conv_t"][:, c, :],
                     lhsT=half[x][c][:, k, :],
                     rhs=ident_f32[:],
                     is_transpose=True,
                     start=(k == 0),
-                    stop=(k == K - 1),
+                    stop=(k == left - 1),
                 )
 
         def round_conv(x):
@@ -274,168 +288,181 @@ def tile_multiheadattention820_pa_t_kernel(tc, v, attn_out, dyn_w, dyn_b, out_pr
                 nc.vector.tensor_tensor(out=out_sb[:, b, :], in0=step[j]["acc%d" % b][:], in1=out_bias[:], op=ALU.add)
             nc.sync.dma_start(out=out_rows[:, j, :, :], in_=out_sb[:])
 
-        with tc.tile_pool(name="prep", bufs=1) as prep:
-            dw_raw = prep.tile([P, 2, E], BF16)
-            nc.sync.dma_start(out=dw_raw[:], in_=dyn_w.rearrange("(g p) e -> p g e", p=P))
-            nc.sync.dma_start(out=v_sb[:, PAD_L : PAD_L + V_ROWS, :, :], in_=v_rows[:, 0:V_ROWS, :, :])
-            load_attn(0)
-            db_raw = prep.tile([P, H * K], BF16)
-            nc.sync.dma_start(out=db_raw[:], in_=dyn_b.partition_broadcast(P))
-            nc.sync.dma_start(out=v_sb[1:113, 0:PAD_L, :, :], in_=v_rows[0:112, LC - PAD_L : LC, :, :])
-            nc.sync.dma_start(out=v_sb[113:P, 0:PAD_L, :, :], in_=v_rows[112 : P - 1, LC - PAD_L : LC, :, :])
+        ctx.enter_context(tc.manual_schedule())
+        dw_raw = prep.tile([P, 2, E], BF16)
+        nc.sync.dma_start(out=dw_raw[:], in_=dyn_w.rearrange("(g p) e -> p g e", p=P))
+        nc.sync.dma_start(out=v_sb[:, PAD_L : PAD_L + V_FIRST, :, :], in_=v_rows[:, 0:V_FIRST, :, :])
+        db_raw = prep.tile([P, H * K], BF16)
+        nc.sync.dma_start(out=db_raw[:], in_=dyn_b.partition_broadcast(P))
+        ow_raw = prep.tile([P, CHUNKS, 2 * E], BF16)
+        nc.sync.dma_start(out=ow_raw[:], in_=out_proj_w.rearrange("(g p) k -> p g k", p=P))
+        nc.sync.dma_start(out=v_sb[1:113, 0:PAD_L, :, :], in_=v_rows[0:112, LC - PAD_L : LC, :, :])
+        nc.sync.dma_start(out=v_sb[113:P, 0:PAD_L, :, :], in_=v_rows[112 : P - 1, LC - PAD_L : LC, :, :])
+        for l0, l1 in ((V_FIRST, V_ROWS), (V_ROWS, 2 * V_ROWS)):
+            nc.sync.dma_start(out=v_sb[:, PAD_L + l0 : PAD_L + l1, :, :], in_=v_rows[:, l0:l1, :, :])
+            load_attn(0 if l0 == V_FIRST else J_ATTN)
+        ob_raw = prep.tile([P, E], BF16)
+        nc.sync.dma_start(out=ob_raw[:], in_=out_proj_b.partition_broadcast(P))
+        for l0 in range(2 * V_ROWS, LC, V_ROWS):
             nc.sync.dma_start(
-                out=v_sb[:, PAD_L + V_ROWS : PAD_L + 2 * V_ROWS, :, :], in_=v_rows[:, V_ROWS : 2 * V_ROWS, :, :]
+                out=v_sb[:, PAD_L + l0 : PAD_L + l0 + V_ROWS, :, :], in_=v_rows[:, l0 : l0 + V_ROWS, :, :]
             )
-            load_attn(J_ATTN)
-            ow_raw = prep.tile([P, CHUNKS, 2 * E], BF16)
-            nc.sync.dma_start(out=ow_raw[:], in_=out_proj_w.rearrange("(g p) k -> p g k", p=P))
-            ob_raw = prep.tile([P, E], BF16)
-            nc.sync.dma_start(out=ob_raw[:], in_=out_proj_b.partition_broadcast(P))
-            for l0 in range(2 * V_ROWS, LC, V_ROWS):
-                nc.sync.dma_start(
-                    out=v_sb[:, PAD_L + l0 : PAD_L + l0 + V_ROWS, :, :], in_=v_rows[:, l0 : l0 + V_ROWS, :, :]
-                )
-            nc.sync.dma_start(out=v_sb[0:112, PAD_L + LC : WIN, :, :], in_=v_rows[1:113, 0:PAD_R, :, :])
-            nc.sync.dma_start(out=v_sb[112 : P - 1, PAD_L + LC : WIN, :, :], in_=v_rows[113:P, 0:PAD_R, :, :])
+        nc.sync.dma_start(out=v_sb[0:112, PAD_L + LC : WIN, :, :], in_=v_rows[1:113, 0:PAD_R, :, :])
+        nc.sync.dma_start(out=v_sb[112 : P - 1, PAD_L + LC : WIN, :, :], in_=v_rows[113:P, 0:PAD_R, :, :])
+        nc.sync.dma_start(out=v_sb[P - 1 : P, PAD_L + LC : WIN, :, :], in_=v_sb[0:1, 0:PAD_R, :, :])
 
-            nc.vector.tensor_copy(out=dyn_bias[:], in_=db_raw[:])
-            dw_grp = prep.tile([P, H * K, PACK], BF16, align_bytes=64)
-            dw_words = dw_raw[:].bitcast(F32)
-            dw_bank = flip_ps.tile([P, 2, 2 * P], F32, tag="flip", name="flip_bank")
+        dw_grp = prep.tile([P, H * K, PACK], BF16, align_bytes=64)
+        dw_words = dw_raw[:].bitcast(F32)
+        dw_bank = flip_ps.tile([P, 2, 2 * P], F32, tag="flip", name="flip_bank")
+        for g in range(2):
+            transpose_words(nc, dw_bank[:, :, g * P : (g + 1) * P], dw_words[:, g, :], ident_f32)
+        nc.vector.tensor_copy(out=dw_grp[:].bitcast(F32), in_=dw_bank[:].rearrange("q u n -> q n u"))
+        nc.vector.quantize_mx(
+            out=dw_codes[:].bitcast(FP8X4), scales=dw_scales[:], in_=dw_grp[:].rearrange("q n t -> q (n t)")
+        )
+        nc.scalar.copy(out=dyn_bias[:], in_=db_raw[:])
+
+        w1_grp = prep.tile([P, E, PACK], BF16, align_bytes=64)
+        w2_grp = prep.tile([P, E, PACK], BF16, align_bytes=64)
+        ow_words = ow_raw[:].bitcast(F32)
+
+        def group_w1(pair):
+            cols = slice(pair * 2 * P, (pair + 1) * 2 * P)
+            bank = out_ps.tile([P, 2, 2 * P], F32, tag="acc0", name="acc0")
             for g in range(2):
-                transpose_words(nc, dw_bank[:, :, g * P : (g + 1) * P], dw_words[:, g, :], ident_f32)
-            nc.vector.tensor_copy(out=dw_grp[:].bitcast(F32), in_=dw_bank[:].rearrange("q u n -> q n u"))
-            nc.vector.quantize_mx(
-                out=dw_codes[:].bitcast(FP8X4), scales=dw_scales[:], in_=dw_grp[:].rearrange("q n t -> q (n t)")
-            )
+                rows = ow_words[:, 2 * pair + g, 0:WORDS]
+                transpose_words(nc, bank[:, :, g * P : (g + 1) * P], rows, ident_f32)
+            nc.vector.tensor_copy(out=w1_grp[:, cols, :].bitcast(F32), in_=bank[:].rearrange("q u n -> q n u"))
 
-            for j in range(2):
-                for name in ("v", "a"):
-                    flip_input(j, name)
-                    group_input(j, name)
-                    quantise_input(j, name)
-                logits_of(j)
-                if j == 0:
-                    bias_and_top(0)
-                    each_head(0, ALU.subtract, "top")
-                    exponentials(0)
-                    inverse_sums(0)
-                    each_head(0, ALU.mult, "inverse")
-            flip_input(2, "v")
-            group_input(2, "v")
-            flip_taps(0)
-            copy_flipped_taps(0)
-            flip_taps_back(0)
+        def group_w2(pair):
+            cols = slice(pair * 2 * P, (pair + 1) * 2 * P)
+            bank = out_ps.tile([P, PACK, 2 * P], BF16, tag="acc1", name="acc1")
+            for g in range(2):
+                for c in range(CHUNKS):
+                    nc.tensor.transpose(
+                        bank[:, c, g * P : (g + 1) * P],
+                        ow_raw[:, 2 * pair + g, E + c * P : E + (c + 1) * P],
+                        ident_bf16[:],
+                    )
+            nc.scalar.copy(out=w2_grp[:, cols, :], in_=bank[:].rearrange("q c n -> q n c"))
 
-            nc.vector.tensor_copy(out=out_bias[:], in_=ob_raw[:])
-            w1_grp = prep.tile([P, E, PACK], BF16, align_bytes=64)
-            w2_grp = prep.tile([P, E, PACK], BF16, align_bytes=64)
-            ow_words = ow_raw[:].bitcast(F32)
-            for pair in range(2):
-                cols = slice(pair * 2 * P, (pair + 1) * 2 * P)
-                w1_bank = out_ps.tile([P, 2, 2 * P], F32, tag="acc0")
-                w2_bank = out_ps.tile([P, PACK, 2 * P], BF16, tag="acc1")
-                for g in range(2):
-                    rows = 2 * pair + g
-                    transpose_words(nc, w1_bank[:, :, g * P : (g + 1) * P], ow_words[:, rows, 0:WORDS], ident_f32)
-                    for c in range(CHUNKS):
-                        nc.tensor.transpose(
-                            w2_bank[:, c, g * P : (g + 1) * P],
-                            ow_raw[:, rows, E + c * P : E + (c + 1) * P],
-                            ident_bf16[:],
-                        )
-                nc.vector.tensor_copy(
-                    out=w1_grp[:, cols, :].bitcast(F32), in_=w1_bank[:].rearrange("q u n -> q n u")
-                )
-                nc.vector.tensor_copy(out=w2_grp[:, cols, :], in_=w2_bank[:].rearrange("q c n -> q n c"))
-            nc.vector.quantize_mx(
-                out=w1_codes[:].bitcast(FP8X4), scales=w1_scales[:], in_=w1_grp[:].rearrange("q n t -> q (n t)")
-            )
-            nc.vector.quantize_mx(
-                out=w2_codes[:].bitcast(FP8X4), scales=w2_scales[:], in_=w2_grp[:].rearrange("q n t -> q (n t)")
-            )
+        flip_input(0, "v")
+        group_input(0, "v")
+        quantise_input(0, "v")
+        logits_of(0)
+        group_w1(0)
+        bias_and_top(0)
+        flip_input(1, "v")
+        group_input(1, "v")
+        each_head(0, ALU.subtract, "top")
+        exponentials(0)
+        quantise_input(1, "v")
+        group_w1(1)
+        logits_of(1)
+        inverse_sums(0)
+        each_head(0, ALU.mult, "inverse")
+        group_w2(0)
+        group_w2(1)
+        nc.gpsimd.tensor_copy(out=out_bias[:], in_=ob_raw[:])
+        nc.vector.quantize_mx(
+            out=w1_codes[:].bitcast(FP8X4), scales=w1_scales[:], in_=w1_grp[:].rearrange("q n t -> q (n t)")
+        )
+        flip_taps(0)
+        copy_flipped_taps(0)
+        flip_taps_back(0)
+        nc.vector.quantize_mx(
+            out=w2_codes[:].bitcast(FP8X4), scales=w2_scales[:], in_=w2_grp[:].rearrange("q n t -> q (n t)")
+        )
+        for j in range(2):
+            flip_input(j, "a")
+            group_input(j, "a")
+            quantise_input(j, "a")
+        flip_input(2, "v")
+        group_input(2, "v")
 
-        prods = ctx.enter_context(tc.tile_pool(name="prods", bufs=2, reuse_waits="tile"))
-
-        with tc.manual_schedule():
-            for x in range(HALF_STEPS + 4):
-                j, b = divmod(x, B)
-                products = x < HALF_STEPS
-                additions = 1 <= x <= HALF_STEPS
-                rounding = 2 <= x < HALF_STEPS + 2
-                softmax_next = j + 1 < LC
-                inputs_after = j + 2 < LC
+        for x in range(HALF_STEPS + 4):
+            j, b = divmod(x, B)
+            products = x < HALF_STEPS
+            additions = 1 <= x <= HALF_STEPS
+            rounding = 2 <= x < HALF_STEPS + 2
+            softmax_next = j + 1 < LC
+            inputs_after = j + 2 < LC
+            if products:
+                half[x] = {}
+                for c in range(CHUNKS):
+                    new_products(x, c)
+            if b == 0:
+                if j % J_ATTN == 0 and j + 4 < LC:
+                    load_attn(j + 4)
+                if inputs_after:
+                    flip_input(j + 2, "a")
+                if softmax_next:
+                    bias_and_top(j + 1)
                 if products:
-                    half[x] = {}
+                    vector_products(x, VECTOR_CHUNKS[0])
+                    gpsimd_products(x, 0)
+                    scalar_products(x, SCALAR_CHUNK, (0,))
+                if softmax_next:
+                    each_head(j + 1, ALU.subtract, "top")
+                if rounding:
+                    round_conv(x - 2)
+                if inputs_after:
+                    group_input(j + 2, "a")
+                if softmax_next:
+                    exponentials(j + 1)
+                if inputs_after:
+                    quantise_input(j + 2, "v")
+                    quantise_input(j + 2, "a")
+                if 0 <= j - 2 < LC:
+                    quantise_conv(j - 2)
+                if products:
+                    for h in range(1, GPSIMD_HEADS):
+                        gpsimd_products(x, h)
+                if softmax_next:
+                    inverse_sums(j + 1)
+                    each_head(j + 1, ALU.mult, "inverse")
+                if additions:
                     for c in range(CHUNKS):
-                        new_products(x, c)
-                if b == 0:
-                    if j % J_ATTN == 0 and j + 4 < LC:
-                        load_attn(j + 4)
-                    if inputs_after:
-                        flip_input(j + 2, "a")
-                    if softmax_next:
-                        bias_and_top(j + 1)
-                    if products:
-                        vector_products(x, VECTOR_CHUNKS[0])
-                        gpsimd_products(x, 0)
-                        scalar_products(x, SCALAR_CHUNK, (0,))
-                    if softmax_next:
-                        each_head(j + 1, ALU.subtract, "top")
-                    if rounding:
-                        round_conv(x - 2)
-                    if inputs_after:
-                        group_input(j + 2, "a")
-                    if softmax_next:
-                        exponentials(j + 1)
-                    if inputs_after:
-                        quantise_input(j + 2, "v")
-                        quantise_input(j + 2, "a")
-                    if 0 <= j - 2 < LC:
-                        quantise_conv(j - 2)
-                    if softmax_next:
-                        inverse_sums(j + 1)
-                        each_head(j + 1, ALU.mult, "inverse")
-                    if additions:
-                        for c in range(CHUNKS):
-                            add_up(x - 1, c)
-                    if products:
-                        vector_products(x, VECTOR_CHUNKS[1])
-                        for h in range(1, GPSIMD_HEADS):
-                            gpsimd_products(x, h)
-                        scalar_products(x, SCALAR_CHUNK, (1, 2, 3))
-                        scalar_products(x, SHARED_CHUNK, range(GPSIMD_HEADS, HEADS_PER_CHUNK))
-                    if 0 <= j - 2 < LC:
-                        project(j - 2)
-                    if inputs_after:
-                        logits_of(j + 2)
-                else:
-                    if softmax_next:
-                        flip_taps(j + 1)
-                    if products:
-                        vector_products(x, VECTOR_CHUNKS[0])
-                        scalar_products(x, SCALAR_CHUNK, (0,))
-                    if additions:
-                        add_up(x - 1, 0)
-                    if softmax_next:
-                        copy_flipped_taps(j + 1)
-                        flip_taps_back(j + 1)
-                    if rounding:
-                        round_conv(x - 2)
-                    if 0 <= j - 2 < LC:
-                        store(j - 2)
-                    if products:
-                        vector_products(x, VECTOR_CHUNKS[1])
-                        scalar_products(x, SCALAR_CHUNK, (1, 2))
-                        for h in range(GPSIMD_HEADS):
-                            gpsimd_products(x, h)
-                    if j + 3 < LC:
-                        flip_input(j + 3, "v")
-                    if additions:
-                        for c in range(1, CHUNKS):
-                            add_up(x - 1, c)
-                    if j + 3 < LC:
-                        group_input(j + 3, "v")
-                    if products:
-                        scalar_products(x, SCALAR_CHUNK, (3,))
-                        scalar_products(x, SHARED_CHUNK, range(GPSIMD_HEADS, HEADS_PER_CHUNK))
+                        add_up(x - 1, c)
+                if products:
+                    vector_products(x, VECTOR_CHUNKS[1])
+                    scalar_products(x, SCALAR_CHUNK, (1, 2, 3))
+                    scalar_products(x, SHARED_CHUNK, range(GPSIMD_HEADS, HEADS_PER_CHUNK))
+                if 0 <= j - 2 < LC:
+                    project(j - 2)
+                if inputs_after:
+                    logits_of(j + 2)
+            else:
+                if softmax_next:
+                    flip_taps(j + 1)
+                if products:
+                    gpsimd_products(x, 0)
+                if additions:
+                    gpsimd_fold(x - 1)
+                if products:
+                    vector_products(x, VECTOR_CHUNKS[0])
+                    scalar_products(x, SCALAR_CHUNK, (0,))
+                if additions:
+                    add_up(x - 1, 0)
+                if softmax_next:
+                    copy_flipped_taps(j + 1)
+                    flip_taps_back(j + 1)
+                if rounding:
+                    round_conv(x - 2)
+                if 0 <= j - 2 < LC:
+                    store(j - 2)
+                if products:
+                    vector_products(x, VECTOR_CHUNKS[1])
+                    scalar_products(x, SCALAR_CHUNK, (1, 2))
+                    for h in range(1, GPSIMD_HEADS):
+                        gpsimd_products(x, h)
+                if j + 3 < LC:
+                    flip_input(j + 3, "v")
+                if additions:
+                    for c in range(1, CHUNKS):
+                        add_up(x - 1, c)
+                if j + 3 < LC:
+                    group_input(j + 3, "v")
+                if products:
+                    scalar_products(x, SCALAR_CHUNK, (3,))
+                    scalar_products(x, SHARED_CHUNK, range(GPSIMD_HEADS, HEADS_PER_CHUNK))

@@ -162,24 +162,15 @@ def tile_multiheadattention820_pa_t_kernel(tc, v, attn_out, dyn_w, dyn_b, out_pr
             nc.vector.reciprocal(out=inverse[:], in_=total[:])
             step[j]["inverse"] = inverse
 
-        def flip_taps(j):
-            bank = flip_ps.tile([P, B, P], F32, tag="flip", name="flip_bank")
-            for b in range(B):
-                rows = step[j]["taps"][:, b, VECTOR_HEADS, :].rearrange("p h k -> p (h k)")
-                nc.tensor.transpose(bank[:, b, :], rows, ident_f32[:])
-            step[j]["taps_bank"] = bank
-
-        def copy_flipped_taps(j):
-            flipped = work.tile([P, B, P], F32, tag="flipped", bufs=1)
-            nc.scalar.copy(out=flipped[:], in_=step[j]["taps_bank"][:])
-            step[j]["flipped"] = flipped
-
-        def flip_taps_back(j):
+        def taps_to_psum(j):
             taps = taps_ps.tile([P, B, P // K, K], F32, tag="taps_ps", name="taps_bank")
-            for b in range(B):
-                nc.tensor.transpose(
-                    taps[:, b, :, :].rearrange("p h k -> p (h k)"), step[j]["flipped"][:, b, :], ident_f32[:]
-                )
+            nc.tensor.matmul(
+                out=taps[:].rearrange("p b h k -> p b (h k)"),
+                lhsT=ident_f32[:],
+                rhs=step[j]["taps"][:, :, VECTOR_HEADS, :].rearrange("p b h k -> p b (h k)"),
+                start=True,
+                stop=True,
+            )
             step[j]["taps_ps"] = taps
 
         def new_products(x, c):
@@ -221,24 +212,17 @@ def tile_multiheadattention820_pa_t_kernel(tc, v, attn_out, dyn_w, dyn_b, out_pr
             head = SHARED_CHUNK * HEADS_PER_CHUNK + h
             wide_products(nc.gpsimd, step[j]["taps"][:, b, head : head + 1, :], x, SHARED_CHUNK, h, 1)
 
-        def gpsimd_fold(x):
-            prod = half[x][SHARED_CHUNK]
-            nc.gpsimd.tensor_tensor(
-                out=prod[:, 0 : K // 2, :], in0=prod[:, 0 : K // 2, :], in1=prod[:, K // 2 : K, :], op=ALU.add
-            )
-
         def add_up(x, c):
             if c == 0:
                 half[x]["conv_t"] = conv_ps.tile([P, CHUNKS, P], F32, tag="conv_t", name="conv_t")
-            left = K // 2 if c == SHARED_CHUNK and x % B == 0 else K
-            for k in range(left):
+            for k in range(K):
                 nc.tensor.matmul(
                     out=half[x]["conv_t"][:, c, :],
                     lhsT=half[x][c][:, k, :],
                     rhs=ident_f32[:],
                     is_transpose=True,
                     start=(k == 0),
-                    stop=(k == left - 1),
+                    stop=(k == K - 1),
                 )
 
         def round_conv(x):
@@ -367,9 +351,7 @@ def tile_multiheadattention820_pa_t_kernel(tc, v, attn_out, dyn_w, dyn_b, out_pr
         nc.vector.quantize_mx(
             out=w1_codes[:].bitcast(FP8X4), scales=w1_scales[:], in_=w1_grp[:].rearrange("q n t -> q (n t)")
         )
-        flip_taps(0)
-        copy_flipped_taps(0)
-        flip_taps_back(0)
+        taps_to_psum(0)
         nc.vector.quantize_mx(
             out=w2_codes[:].bitcast(FP8X4), scales=w2_scales[:], in_=w2_grp[:].rearrange("q n t -> q (n t)")
         )
@@ -394,25 +376,17 @@ def tile_multiheadattention820_pa_t_kernel(tc, v, attn_out, dyn_w, dyn_b, out_pr
             if b == 0:
                 if j % J_ATTN == 0 and j + 4 < LC:
                     load_attn(j + 4)
-                if inputs_after:
-                    flip_input(j + 2, "a")
                 if softmax_next:
                     bias_and_top(j + 1)
                 if products:
                     vector_products(x, VECTOR_CHUNKS[0])
                     gpsimd_products(x, 0)
-                    scalar_products(x, SCALAR_CHUNK, (0,))
+                    scalar_products(x, SCALAR_CHUNK, (0, 1, 2))
                 if softmax_next:
                     each_head(j + 1, ALU.subtract, "top")
-                if rounding:
-                    round_conv(x - 2)
-                if inputs_after:
-                    group_input(j + 2, "a")
-                if softmax_next:
                     exponentials(j + 1)
                 if inputs_after:
                     quantise_input(j + 2, "v")
-                    quantise_input(j + 2, "a")
                 if 0 <= j - 2 < LC:
                     quantise_conv(j - 2)
                 if products:
@@ -422,47 +396,53 @@ def tile_multiheadattention820_pa_t_kernel(tc, v, attn_out, dyn_w, dyn_b, out_pr
                     inverse_sums(j + 1)
                     each_head(j + 1, ALU.mult, "inverse")
                 if additions:
-                    for c in range(CHUNKS):
-                        add_up(x - 1, c)
+                    add_up(x - 1, 0)
+                    add_up(x - 1, 1)
+                if inputs_after:
+                    flip_input(j + 2, "a")
+                if additions:
+                    add_up(x - 1, 2)
+                    add_up(x - 1, 3)
                 if products:
                     vector_products(x, VECTOR_CHUNKS[1])
-                    scalar_products(x, SCALAR_CHUNK, (1, 2, 3))
+                if rounding:
+                    round_conv(x - 2)
+                if products:
+                    scalar_products(x, SCALAR_CHUNK, (3,))
+                if inputs_after:
+                    group_input(j + 2, "a")
+                if products:
                     scalar_products(x, SHARED_CHUNK, range(GPSIMD_HEADS, HEADS_PER_CHUNK))
                 if 0 <= j - 2 < LC:
                     project(j - 2)
                 if inputs_after:
                     logits_of(j + 2)
             else:
-                if softmax_next:
-                    flip_taps(j + 1)
-                if products:
-                    gpsimd_products(x, 0)
-                if additions:
-                    gpsimd_fold(x - 1)
                 if products:
                     vector_products(x, VECTOR_CHUNKS[0])
-                    scalar_products(x, SCALAR_CHUNK, (0,))
+                    scalar_products(x, SCALAR_CHUNK, (0, 1))
                 if additions:
                     add_up(x - 1, 0)
+                    add_up(x - 1, 1)
                 if softmax_next:
-                    copy_flipped_taps(j + 1)
-                    flip_taps_back(j + 1)
-                if rounding:
-                    round_conv(x - 2)
-                if 0 <= j - 2 < LC:
-                    store(j - 2)
-                if products:
-                    vector_products(x, VECTOR_CHUNKS[1])
-                    scalar_products(x, SCALAR_CHUNK, (1, 2))
-                    for h in range(1, GPSIMD_HEADS):
-                        gpsimd_products(x, h)
+                    taps_to_psum(j + 1)
                 if j + 3 < LC:
                     flip_input(j + 3, "v")
                 if additions:
-                    for c in range(1, CHUNKS):
-                        add_up(x - 1, c)
+                    add_up(x - 1, 2)
+                    add_up(x - 1, 3)
+                if inputs_after:
+                    quantise_input(j + 2, "a")
+                if 0 <= j - 2 < LC:
+                    store(j - 2)
+                if rounding:
+                    round_conv(x - 2)
+                if products:
+                    vector_products(x, VECTOR_CHUNKS[1])
+                    scalar_products(x, SCALAR_CHUNK, (2, 3))
+                    for h in range(GPSIMD_HEADS):
+                        gpsimd_products(x, h)
                 if j + 3 < LC:
                     group_input(j + 3, "v")
                 if products:
-                    scalar_products(x, SCALAR_CHUNK, (3,))
                     scalar_products(x, SHARED_CHUNK, range(GPSIMD_HEADS, HEADS_PER_CHUNK))

@@ -111,6 +111,11 @@ def tile_multiheadattention820_pa_t_kernel(tc, v, attn_out, dyn_w, dyn_b, out_pr
             step[j][name + "_codes"] = codes
             step[j][name + "_scales"] = scales
 
+        def whole_input(j, name):
+            flip_input(j, name)
+            group_input(j, name)
+            quantise_input(j, name)
+
         def logits_of(j):
             logits = logit_ps.tile([P, B, H * K], F32, tag="logits")
             for b in range(B):
@@ -212,17 +217,27 @@ def tile_multiheadattention820_pa_t_kernel(tc, v, attn_out, dyn_w, dyn_b, out_pr
             head = SHARED_CHUNK * HEADS_PER_CHUNK + h
             wide_products(nc.gpsimd, step[j]["taps"][:, b, head : head + 1, :], x, SHARED_CHUNK, h, 1)
 
+        def folded(x):
+            return x % B == 0
+
+        def gpsimd_fold(x):
+            prod = half[x][SHARED_CHUNK]
+            nc.gpsimd.tensor_tensor(
+                out=prod[:, 0 : K // 2, :], in0=prod[:, 0 : K // 2, :], in1=prod[:, K // 2 : K, :], op=ALU.add
+            )
+
         def add_up(x, c):
-            if c == 0:
+            if c == VECTOR_CHUNKS[0]:
                 half[x]["conv_t"] = conv_ps.tile([P, CHUNKS, P], F32, tag="conv_t", name="conv_t")
-            for k in range(K):
+            left = K // 2 if c == SHARED_CHUNK and folded(x) else K
+            for k in range(left):
                 nc.tensor.matmul(
                     out=half[x]["conv_t"][:, c, :],
                     lhsT=half[x][c][:, k, :],
                     rhs=ident_f32[:],
                     is_transpose=True,
                     start=(k == 0),
-                    stop=(k == K - 1),
+                    stop=(k == left - 1),
                 )
 
         def round_conv(x):
@@ -330,9 +345,7 @@ def tile_multiheadattention820_pa_t_kernel(tc, v, attn_out, dyn_w, dyn_b, out_pr
                     )
             nc.scalar.copy(out=w2_grp[:, cols, :], in_=bank[:].rearrange("q c n -> q n c"))
 
-        flip_input(0, "v")
-        group_input(0, "v")
-        quantise_input(0, "v")
+        whole_input(0, "v")
         logits_of(0)
         group_w1(0)
         bias_and_top(0)
@@ -347,7 +360,6 @@ def tile_multiheadattention820_pa_t_kernel(tc, v, attn_out, dyn_w, dyn_b, out_pr
         each_head(0, ALU.mult, "inverse")
         group_w2(0)
         group_w2(1)
-        nc.gpsimd.tensor_copy(out=out_bias[:], in_=ob_raw[:])
         nc.vector.quantize_mx(
             out=w1_codes[:].bitcast(FP8X4), scales=w1_scales[:], in_=w1_grp[:].rearrange("q n t -> q (n t)")
         )
@@ -355,10 +367,6 @@ def tile_multiheadattention820_pa_t_kernel(tc, v, attn_out, dyn_w, dyn_b, out_pr
         nc.vector.quantize_mx(
             out=w2_codes[:].bitcast(FP8X4), scales=w2_scales[:], in_=w2_grp[:].rearrange("q n t -> q (n t)")
         )
-        for j in range(2):
-            flip_input(j, "a")
-            group_input(j, "a")
-            quantise_input(j, "a")
         flip_input(2, "v")
         group_input(2, "v")
 
@@ -374,8 +382,6 @@ def tile_multiheadattention820_pa_t_kernel(tc, v, attn_out, dyn_w, dyn_b, out_pr
                 for c in range(CHUNKS):
                     new_products(x, c)
             if b == 0:
-                if j % J_ATTN == 0 and j + 4 < LC:
-                    load_attn(j + 4)
                 if softmax_next:
                     bias_and_top(j + 1)
                 if products:
@@ -396,8 +402,8 @@ def tile_multiheadattention820_pa_t_kernel(tc, v, attn_out, dyn_w, dyn_b, out_pr
                     inverse_sums(j + 1)
                     each_head(j + 1, ALU.mult, "inverse")
                 if additions:
-                    add_up(x - 1, 0)
                     add_up(x - 1, 1)
+                    add_up(x - 1, 0)
                 if inputs_after:
                     flip_input(j + 2, "a")
                 if additions:
@@ -415,21 +421,27 @@ def tile_multiheadattention820_pa_t_kernel(tc, v, attn_out, dyn_w, dyn_b, out_pr
                     scalar_products(x, SHARED_CHUNK, range(GPSIMD_HEADS, HEADS_PER_CHUNK))
                 if 0 <= j - 2 < LC:
                     project(j - 2)
-                if inputs_after:
-                    logits_of(j + 2)
+                if j == 0:
+                    nc.gpsimd.tensor_copy(out=out_bias[:], in_=ob_raw[:])
+                    whole_input(0, "a")
             else:
+                if additions and folded(x - 1):
+                    gpsimd_fold(x - 1)
                 if products:
                     vector_products(x, VECTOR_CHUNKS[0])
                     scalar_products(x, SCALAR_CHUNK, (0, 1))
                 if additions:
-                    add_up(x - 1, 0)
                     add_up(x - 1, 1)
-                if softmax_next:
-                    taps_to_psum(j + 1)
+                    add_up(x - 1, 0)
                 if j + 3 < LC:
                     flip_input(j + 3, "v")
                 if additions:
                     add_up(x - 1, 2)
+                if softmax_next:
+                    taps_to_psum(j + 1)
+                if inputs_after:
+                    logits_of(j + 2)
+                if additions:
                     add_up(x - 1, 3)
                 if inputs_after:
                     quantise_input(j + 2, "a")
@@ -446,3 +458,7 @@ def tile_multiheadattention820_pa_t_kernel(tc, v, attn_out, dyn_w, dyn_b, out_pr
                     group_input(j + 3, "v")
                 if products:
                     scalar_products(x, SHARED_CHUNK, range(GPSIMD_HEADS, HEADS_PER_CHUNK))
+                if j == 0:
+                    whole_input(1, "a")
+                if j % J_ATTN == 0 and j + 2 * J_ATTN < LC:
+                    load_attn(j + 2 * J_ATTN)

from contextlib import ExitStack

import concourse.mybir as mybir
from concourse.masks import make_identity

F32 = mybir.dt.float32
BF16 = mybir.dt.bfloat16
U32 = mybir.dt.uint32
U8 = mybir.dt.uint8
FP8X4 = mybir.dt.float8_e4m3fn_x4
ALU = mybir.AluOpType
ACT = mybir.ActivationFunctionType
AXIS_X = mybir.AxisListType.X

T, B, E, H, K = 4096, 2, 512, 16, 16
R = E // H
P = 128
PACK = 4
LC = T // P
PAD_L = K // 2
PAD_R = K - 1 - PAD_L
WIN = LC + K - 1
CHUNKS = E // P
HEADS_PER_CHUNK = P // R
WORDS = E // 2
HALF_STEPS = B * LC
J_ATTN = 2
V_ROWS = 8
V_FIRST = 2
SCALAR_CHUNK, VECTOR_CHUNKS, SHARED_CHUNK = 0, (1, 2), 3
GPSIMD_HEADS = 3
VECTOR_HEADS = slice(4, 12)

FLOPS = 2 * T * B * (E * H * K + 2 * E * E + E * K)


def transpose_words(nc, bank, rows_as_words, ident_f32):
    for u in range(2):
        nc.tensor.transpose(bank[:, u, :], rows_as_words[:, u * P : (u + 1) * P], ident_f32[:])


def tile_multiheadattention820_pa_t_kernel(tc, v, attn_out, dyn_w, dyn_b, out_proj_w, out_proj_b, out):
    nc = tc.nc
    v_rows = v.rearrange("(p l) b e -> p l b e", l=LC)
    attn_rows = attn_out.rearrange("(p l) b e -> p l b e", l=LC)
    out_rows = out.rearrange("(p l) b o -> p l b o", l=LC)

    with ExitStack() as ctx:
        keep = ctx.enter_context(tc.tile_pool(name="keep", bufs=1))
        loads = ctx.enter_context(tc.tile_pool(name="loads", bufs=2))
        work = ctx.enter_context(tc.tile_pool(name="work", bufs=2))
        prep = ctx.enter_context(tc.tile_pool(name="prep", bufs=1))
        prods = ctx.enter_context(tc.tile_pool(name="prods", bufs=2))
        flip_ps = ctx.enter_context(tc.psum_pool(name="flip_ps", bufs=1))
        logit_ps = ctx.enter_context(tc.psum_pool(name="logit_ps", bufs=1))
        taps_ps = ctx.enter_context(tc.psum_pool(name="taps_ps", bufs=2))
        conv_ps = ctx.enter_context(tc.psum_pool(name="conv_ps", bufs=2))
        out_ps = ctx.enter_context(tc.psum_pool(name="out_ps", bufs=1))

        v_sb = keep.tile([P, WIN, B, E], BF16)
        ident_f32 = keep.tile([P, P], F32)
        make_identity(nc, ident_f32[:])
        ident_bf16 = keep.tile([P, P], BF16)
        make_identity(nc, ident_bf16[:])
        nc.gpsimd.memset(v_sb[0:1, 0:PAD_L, :, :].rearrange("p x b e -> p (x b e)").bitcast(F32), 0.0)

        dw_codes = keep.tile([P, H * K], U32, align_bytes=64)
        dw_scales = keep.tile([P, H * K], U8, align_bytes=64)
        w1_codes = keep.tile([P, E], U32, align_bytes=64)
        w1_scales = keep.tile([P, E], U8, align_bytes=64)
        w2_codes = keep.tile([P, E], U32, align_bytes=64)
        w2_scales = keep.tile([P, E], U8, align_bytes=64)
        dyn_bias = keep.tile([P, H * K], F32)
        out_bias = keep.tile([P, E], F32)

        attn_tiles = {}
        step = {}
        half = {}

        def load_attn(j):
            attn_tiles[j] = loads.tile([P, J_ATTN, B, E], BF16, tag="attn", name="attn_sb")
            nc.sync.dma_start(out=attn_tiles[j][:], in_=attn_rows[:, j : j + J_ATTN, :, :])

        def flip_input(j, name):
            step.setdefault(j, {})
            if name == "v":
                rows = v_sb[:, PAD_L + j, :, :].bitcast(F32)
            else:
                rows = attn_tiles[j - j % J_ATTN][:, j % J_ATTN, :, :].bitcast(F32)
            bank = flip_ps.tile([P, B, 2, P], F32, tag="flip", name="flip_bank")
            for b in range(B):
                transpose_words(nc, bank[:, b, :, :], rows[:, b, :], ident_f32)
            step[j][name + "_bank"] = bank

        def group_input(j, name):
            grouped = work.tile([P, B, P, PACK], BF16, align_bytes=64, tag=name + "_grp", name=name + "_grp")
            nc.scalar.copy(
                out=grouped[:].bitcast(F32), in_=step[j][name + "_bank"][:].rearrange("q b u n -> q b n u")
            )
            step[j][name + "_grp"] = grouped

        def quantise_input(j, name):
            slots = 2 if name == "v" else 5
            codes = work.tile([P, B * P], U32, align_bytes=64, tag=name + "_codes", name=name + "_codes", bufs=slots)
            scales = work.tile([P, B * P], U8, align_bytes=64, tag=name + "_scales", name=name + "_scales", bufs=slots)
            nc.vector.quantize_mx(
                out=codes[:].bitcast(FP8X4),
                scales=scales[:],
                in_=step[j][name + "_grp"][:].rearrange("q b n t -> q (b n t)"),
            )
            step[j][name + "_codes"] = codes
            step[j][name + "_scales"] = scales

        def whole_input(j, name):
            flip_input(j, name)
            group_input(j, name)
            quantise_input(j, name)

        def logits_of(j):
            logits = logit_ps.tile([P, B, H * K], F32, tag="logits")
            for b in range(B):
                tokens = slice(b * P, (b + 1) * P)
                nc.tensor.matmul_mx(
                    out=logits[:, b, :],
                    lhsT=step[j]["v_codes"][:, tokens].bitcast(FP8X4),
                    lhsT_scale=step[j]["v_scales"][:, tokens],
                    rhs=dw_codes[:].bitcast(FP8X4),
                    rhs_scale=dw_scales[:],
                    start=True,
                    stop=True,
                )
            step[j]["logits"] = logits

        def by_head(taps):
            return taps[:].rearrange("p b h k -> p (b h) k")

        def bias_and_top(j):
            taps = work.tile([P, B, H, K], F32, tag="taps")
            nc.vector.tensor_tensor(
                out=taps[:].rearrange("p b h k -> p b (h k)"),
                in0=step[j]["logits"][:],
                in1=dyn_bias[:].unsqueeze(1).to_broadcast([P, B, H * K]),
                op=ALU.add,
            )
            top = work.tile([P, B * H], F32, tag="top")
            nc.vector.tensor_reduce(out=top[:], in_=by_head(taps), axis=AXIS_X, op=ALU.max)
            step[j]["taps"] = taps
            step[j]["top"] = top

        def each_head(j, op, per_head):
            taps = step[j]["taps"]
            nc.gpsimd.tensor_tensor(
                out=by_head(taps),
                in0=by_head(taps),
                in1=step[j][per_head][:].unsqueeze(2).to_broadcast([P, B * H, K]),
                op=op,
            )

        def exponentials(j):
            flat = step[j]["taps"][:].rearrange("p b h k -> p (b h k)")
            nc.scalar.activation(out=flat, in_=flat, func=ACT.Exp)

        def inverse_sums(j):
            total = work.tile([P, B * H], F32, tag="total")
            nc.vector.tensor_reduce(out=total[:], in_=by_head(step[j]["taps"]), axis=AXIS_X, op=ALU.add)
            inverse = work.tile([P, B * H], F32, tag="inverse")
            nc.vector.reciprocal(out=inverse[:], in_=total[:])
            step[j]["inverse"] = inverse

        def taps_to_psum(j):
            taps = taps_ps.tile([P, B, P // K, K], F32, tag="taps_ps", name="taps_bank")
            nc.tensor.matmul(
                out=taps[:].rearrange("p b h k -> p b (h k)"),
                lhsT=ident_f32[:],
                rhs=step[j]["taps"][:, :, VECTOR_HEADS, :].rearrange("p b h k -> p b (h k)"),
                start=True,
                stop=True,
            )
            step[j]["taps_ps"] = taps

        def new_products(x, c):
            half[x][c] = prods.tile([P, K, P], F32, tag="prod%d" % c, name="prod%d" % c)

        def scalar_products(x, c, heads):
            j, b = divmod(x, B)
            prod = half[x][c]
            for h in heads:
                head = c * HEADS_PER_CHUNK + h
                for k in range(K):
                    nc.scalar.activation(
                        out=prod[:, k, h * R : (h + 1) * R],
                        in_=v_sb[:, j + k, b, head * R : (head + 1) * R],
                        func=ACT.Copy,
                        scale=step[j]["taps"][:, b, head, k : k + 1],
                    )

        def wide_products(engine, taps, x, c, first, count):
            j = x // B
            channels = slice(first * R, (first + count) * R)
            head = c * HEADS_PER_CHUNK + first
            engine.tensor_tensor(
                out=half[x][c][:, :, channels].rearrange("p k (h r) -> p k h r", r=R),
                in0=v_sb[:, j : j + K, x % B, head * R : (head + count) * R].rearrange("p k (h r) -> p k h r", r=R),
                in1=taps.rearrange("p h k -> p k h").unsqueeze(3).to_broadcast([P, K, count, R]),
                op=ALU.mult,
            )

        def vector_products(x, c):
            j, b = divmod(x, B)
            first = c * HEADS_PER_CHUNK - VECTOR_HEADS.start
            wide_products(
                nc.vector, step[j]["taps_ps"][:, b, first : first + HEADS_PER_CHUNK, :], x, c, 0, HEADS_PER_CHUNK
            )

        def gpsimd_products(x, h):
            j, b = divmod(x, B)
            head = SHARED_CHUNK * HEADS_PER_CHUNK + h
            wide_products(nc.gpsimd, step[j]["taps"][:, b, head : head + 1, :], x, SHARED_CHUNK, h, 1)

        def folded(x):
            return x % B == 0

        def gpsimd_fold(x):
            prod = half[x][SHARED_CHUNK]
            nc.gpsimd.tensor_tensor(
                out=prod[:, 0 : K // 2, :], in0=prod[:, 0 : K // 2, :], in1=prod[:, K // 2 : K, :], op=ALU.add
            )

        def add_up(x, c):
            if c == VECTOR_CHUNKS[0]:
                half[x]["conv_t"] = conv_ps.tile([P, CHUNKS, P], F32, tag="conv_t", name="conv_t")
            left = K // 2 if c == SHARED_CHUNK and folded(x) else K
            for k in range(left):
                nc.tensor.matmul(
                    out=half[x]["conv_t"][:, c, :],
                    lhsT=half[x][c][:, k, :],
                    rhs=ident_f32[:],
                    is_transpose=True,
                    start=(k == 0),
                    stop=(k == left - 1),
                )

        def round_conv(x):
            j, b = divmod(x, B)
            if b == 0:
                step[j]["conv_grp"] = work.tile([P, B, P, PACK], BF16, align_bytes=64, tag="conv_grp", name="conv_grp", bufs=3)
            nc.scalar.copy(out=step[j]["conv_grp"][:, b, :, :], in_=half[x]["conv_t"][:].rearrange("q c n -> q n c"))

        def quantise_conv(j):
            c_codes = work.tile([P, B * P], U32, align_bytes=64, tag="c_codes")
            c_scales = work.tile([P, B * P], U8, align_bytes=64, tag="c_scales")
            nc.vector.quantize_mx(
                out=c_codes[:].bitcast(FP8X4),
                scales=c_scales[:],
                in_=step[j]["conv_grp"][:].rearrange("q b n t -> q (b n t)"),
            )
            step[j]["c_codes"] = c_codes
            step[j]["c_scales"] = c_scales

        def project(j):
            for b in range(B):
                tokens = slice(b * P, (b + 1) * P)
                acc = out_ps.tile([P, E], F32, tag="acc%d" % b, name="acc%d" % b)
                nc.tensor.matmul_mx(
                    out=acc[:],
                    lhsT=step[j]["a_codes"][:, tokens].bitcast(FP8X4),
                    lhsT_scale=step[j]["a_scales"][:, tokens],
                    rhs=w1_codes[:].bitcast(FP8X4),
                    rhs_scale=w1_scales[:],
                    start=True,
                    stop=False,
                )
                nc.tensor.matmul_mx(
                    out=acc[:],
                    lhsT=step[j]["c_codes"][:, tokens].bitcast(FP8X4),
                    lhsT_scale=step[j]["c_scales"][:, tokens],
                    rhs=w2_codes[:].bitcast(FP8X4),
                    rhs_scale=w2_scales[:],
                    start=False,
                    stop=True,
                )
                step[j]["acc%d" % b] = acc

        def store(j):
            out_sb = work.tile([P, B, E], F32, tag="out_sb")
            for b in range(B):
                nc.vector.tensor_tensor(out=out_sb[:, b, :], in0=step[j]["acc%d" % b][:], in1=out_bias[:], op=ALU.add)
            nc.sync.dma_start(out=out_rows[:, j, :, :], in_=out_sb[:])

        ctx.enter_context(tc.manual_schedule())
        dw_raw = prep.tile([P, 2, E], BF16)
        nc.sync.dma_start(out=dw_raw[:], in_=dyn_w.rearrange("(g p) e -> p g e", p=P))
        nc.sync.dma_start(out=v_sb[:, PAD_L : PAD_L + V_FIRST, :, :], in_=v_rows[:, 0:V_FIRST, :, :])
        db_raw = prep.tile([P, H * K], BF16)
        nc.sync.dma_start(out=db_raw[:], in_=dyn_b.partition_broadcast(P))
        ow_raw = prep.tile([P, CHUNKS, 2 * E], BF16)
        nc.sync.dma_start(out=ow_raw[:], in_=out_proj_w.rearrange("(g p) k -> p g k", p=P))
        nc.sync.dma_start(out=v_sb[1:113, 0:PAD_L, :, :], in_=v_rows[0:112, LC - PAD_L : LC, :, :])
        nc.sync.dma_start(out=v_sb[113:P, 0:PAD_L, :, :], in_=v_rows[112 : P - 1, LC - PAD_L : LC, :, :])
        for l0, l1 in ((V_FIRST, V_ROWS), (V_ROWS, 2 * V_ROWS)):
            nc.sync.dma_start(out=v_sb[:, PAD_L + l0 : PAD_L + l1, :, :], in_=v_rows[:, l0:l1, :, :])
            load_attn(0 if l0 == V_FIRST else J_ATTN)
        ob_raw = prep.tile([P, E], BF16)
        nc.sync.dma_start(out=ob_raw[:], in_=out_proj_b.partition_broadcast(P))
        for l0 in range(2 * V_ROWS, LC, V_ROWS):
            nc.sync.dma_start(
                out=v_sb[:, PAD_L + l0 : PAD_L + l0 + V_ROWS, :, :], in_=v_rows[:, l0 : l0 + V_ROWS, :, :]
            )
        nc.sync.dma_start(out=v_sb[0:112, PAD_L + LC : WIN, :, :], in_=v_rows[1:113, 0:PAD_R, :, :])
        nc.sync.dma_start(out=v_sb[112 : P - 1, PAD_L + LC : WIN, :, :], in_=v_rows[113:P, 0:PAD_R, :, :])
        nc.sync.dma_start(out=v_sb[P - 1 : P, PAD_L + LC : WIN, :, :], in_=v_sb[0:1, 0:PAD_R, :, :])

        dw_grp = prep.tile([P, H * K, PACK], BF16, align_bytes=64)
        dw_words = dw_raw[:].bitcast(F32)
        dw_bank = flip_ps.tile([P, 2, 2 * P], F32, tag="flip", name="flip_bank")
        for g in range(2):
            transpose_words(nc, dw_bank[:, :, g * P : (g + 1) * P], dw_words[:, g, :], ident_f32)
        nc.vector.tensor_copy(out=dw_grp[:].bitcast(F32), in_=dw_bank[:].rearrange("q u n -> q n u"))
        nc.vector.quantize_mx(
            out=dw_codes[:].bitcast(FP8X4), scales=dw_scales[:], in_=dw_grp[:].rearrange("q n t -> q (n t)")
        )
        nc.scalar.copy(out=dyn_bias[:], in_=db_raw[:])

        w1_grp = prep.tile([P, E, PACK], BF16, align_bytes=64)
        w2_grp = prep.tile([P, E, PACK], BF16, align_bytes=64)
        ow_words = ow_raw[:].bitcast(F32)

        def group_w1(pair):
            cols = slice(pair * 2 * P, (pair + 1) * 2 * P)
            bank = out_ps.tile([P, 2, 2 * P], F32, tag="acc0", name="acc0")
            for g in range(2):
                rows = ow_words[:, 2 * pair + g, 0:WORDS]
                transpose_words(nc, bank[:, :, g * P : (g + 1) * P], rows, ident_f32)
            nc.vector.tensor_copy(out=w1_grp[:, cols, :].bitcast(F32), in_=bank[:].rearrange("q u n -> q n u"))

        def group_w2(pair):
            cols = slice(pair * 2 * P, (pair + 1) * 2 * P)
            bank = out_ps.tile([P, PACK, 2 * P], BF16, tag="acc1", name="acc1")
            for g in range(2):
                for c in range(CHUNKS):
                    nc.tensor.transpose(
                        bank[:, c, g * P : (g + 1) * P],
                        ow_raw[:, 2 * pair + g, E + c * P : E + (c + 1) * P],
                        ident_bf16[:],
                    )
            nc.scalar.copy(out=w2_grp[:, cols, :], in_=bank[:].rearrange("q c n -> q n c"))

        whole_input(0, "v")
        logits_of(0)
        group_w1(0)
        bias_and_top(0)
        flip_input(1, "v")
        group_input(1, "v")
        each_head(0, ALU.subtract, "top")
        exponentials(0)
        quantise_input(1, "v")
        group_w1(1)
        logits_of(1)
        inverse_sums(0)
        each_head(0, ALU.mult, "inverse")
        group_w2(0)
        group_w2(1)
        nc.vector.quantize_mx(
            out=w1_codes[:].bitcast(FP8X4), scales=w1_scales[:], in_=w1_grp[:].rearrange("q n t -> q (n t)")
        )
        taps_to_psum(0)
        nc.vector.quantize_mx(
            out=w2_codes[:].bitcast(FP8X4), scales=w2_scales[:], in_=w2_grp[:].rearrange("q n t -> q (n t)")
        )
        flip_input(2, "v")
        group_input(2, "v")

        for x in range(HALF_STEPS + 4):
            j, b = divmod(x, B)
            products = x < HALF_STEPS
            additions = 1 <= x <= HALF_STEPS
            rounding = 2 <= x < HALF_STEPS + 2
            softmax_next = j + 1 < LC
            inputs_after = j + 2 < LC
            if products:
                half[x] = {}
                for c in range(CHUNKS):
                    new_products(x, c)
            if b == 0:
                if softmax_next:
                    bias_and_top(j + 1)
                if products:
                    vector_products(x, VECTOR_CHUNKS[0])
                    gpsimd_products(x, 0)
                    scalar_products(x, SCALAR_CHUNK, (0, 1, 2))
                if softmax_next:
                    each_head(j + 1, ALU.subtract, "top")
                    exponentials(j + 1)
                if inputs_after:
                    quantise_input(j + 2, "v")
                if 0 <= j - 2 < LC:
                    quantise_conv(j - 2)
                if products:
                    for h in range(1, GPSIMD_HEADS):
                        gpsimd_products(x, h)
                if softmax_next:
                    inverse_sums(j + 1)
                    each_head(j + 1, ALU.mult, "inverse")
                if additions:
                    add_up(x - 1, 1)
                    add_up(x - 1, 0)
                if inputs_after:
                    flip_input(j + 2, "a")
                if additions:
                    add_up(x - 1, 2)
                    add_up(x - 1, 3)
                if products:
                    vector_products(x, VECTOR_CHUNKS[1])
                if rounding:
                    round_conv(x - 2)
                if products:
                    scalar_products(x, SCALAR_CHUNK, (3,))
                if inputs_after:
                    group_input(j + 2, "a")
                if products:
                    scalar_products(x, SHARED_CHUNK, range(GPSIMD_HEADS, HEADS_PER_CHUNK))
                if 0 <= j - 2 < LC:
                    project(j - 2)
                if j == 0:
                    nc.gpsimd.tensor_copy(out=out_bias[:], in_=ob_raw[:])
                    whole_input(0, "a")
            else:
                if additions and folded(x - 1):
                    gpsimd_fold(x - 1)
                if products:
                    vector_products(x, VECTOR_CHUNKS[0])
                    scalar_products(x, SCALAR_CHUNK, (0, 1))
                if additions:
                    add_up(x - 1, 1)
                    add_up(x - 1, 0)
                if j + 3 < LC:
                    flip_input(j + 3, "v")
                if additions:
                    add_up(x - 1, 2)
                if softmax_next:
                    taps_to_psum(j + 1)
                if inputs_after:
                    logits_of(j + 2)
                if additions:
                    add_up(x - 1, 3)
                if inputs_after:
                    quantise_input(j + 2, "a")
                if 0 <= j - 2 < LC:
                    store(j - 2)
                if rounding:
                    round_conv(x - 2)
                if products:
                    vector_products(x, VECTOR_CHUNKS[1])
                    scalar_products(x, SCALAR_CHUNK, (2, 3))
                    for h in range(GPSIMD_HEADS):
                        gpsimd_products(x, h)
                if j + 3 < LC:
                    group_input(j + 3, "v")
                if products:
                    scalar_products(x, SHARED_CHUNK, range(GPSIMD_HEADS, HEADS_PER_CHUNK))
                if j == 0:
                    whole_input(1, "a")
                if j % J_ATTN == 0 and j + 2 * J_ATTN < LC:
                    load_attn(j + 2 * J_ATTN)
